import numpy as np
import ml_dtypes


def mxq(x, axis, fmt="e4m3"):
    dtype, down = {"e4m3": (ml_dtypes.float8_e4m3fn, 7), "e5m2": (ml_dtypes.float8_e5m2, 14)}[fmt]
    v = np.moveaxis(np.asarray(x, np.float32).astype(ml_dtypes.bfloat16).astype(np.float64), axis, -1)
    blocks = v.reshape(v.shape[:-1] + (-1, 32))
    amax = np.abs(blocks).max(-1, keepdims=True)
    byte = np.maximum(np.where(amax > 0, np.frexp(amax)[1] - 1 + 127, 0) - down, 1)
    scale = np.exp2(byte - 127.0)
    codes = (blocks / scale).astype(np.float32).astype(dtype).astype(np.float64)
    return np.moveaxis((codes * scale).reshape(v.shape), -1, axis)


WIDE = False


def mx_kscale(k):
    if not WIDE:
        return np.ones(k)
    levels = np.array([10, -10, 5, -5, 0])
    if k % 512:
        return np.exp2(np.random.permutation(np.resize(levels, k // 32))).repeat(32)
    a = np.empty((k // 512, 16))
    for p in range(k // 512):
        a[p, :8] = np.random.permutation(np.resize(levels, 8))
        for g in range(8):
            far = levels[np.abs(levels - a[p, g]) >= 10]
            a[p, g + 8] = far[np.random.randint(len(far))]
    return np.exp2(a.ravel()).repeat(32)


BF16 = ml_dtypes.bfloat16


def bf(x):
    return np.asarray(x, np.float32).astype(BF16)


def f64(x):
    return np.asarray(x).astype(np.float64)


E2M1 = np.array([0.0, 0.5, 1.0, 1.5, 2.0, 3.0, 4.0, 6.0, -0.0, -0.5, -1.0, -1.5, -2.0, -3.0, -4.0, -6.0])


def pack_weight(w, fmt):
    k, n = w.shape
    w = f64(bf(w)).reshape(k // 32, 32, n)
    amax = np.abs(w).max(1)
    if fmt == "e4m3":
        byte = np.frexp(amax)[1] - 1 + 127 - 7
    else:
        mant, ex = np.frexp(amax / 6.0)
        byte = np.where(mant > 0.5, ex, ex - 1) + 127
    byte = np.clip(np.where(amax > 0, byte, 1), 1, 254)
    scaled = (w * np.exp2(127.0 - byte)[:, None, :]).reshape(k, n).astype(np.float32)
    by_word = np.ascontiguousarray(scaled.reshape(k // 512, 128, 4, n).transpose(0, 1, 3, 2))
    if fmt == "e4m3":
        words = by_word.astype(ml_dtypes.float8_e4m3fn).view(np.uint8)
    else:
        c = by_word.astype(ml_dtypes.float4_e2m1fn).view(np.uint8) & 0xF
        words = c[..., 0::2] | (c[..., 1::2] << 4)
    return np.ascontiguousarray(words), np.ascontiguousarray(byte.astype(np.uint8).reshape(k // 512, 16, n))


def unpack_weight(words, scales, fmt):
    g, p, n, _ = words.shape
    if fmt == "e4m3":
        vals = np.ascontiguousarray(words).view(ml_dtypes.float8_e4m3fn).astype(np.float64)
    else:
        nib = np.empty((g, p, n, 4), np.uint8)
        nib[..., 0::2] = words & 0xF
        nib[..., 1::2] = words >> 4
        vals = E2M1[nib]
    vals = vals * np.repeat(np.exp2(scales.astype(np.float64) - 127.0), 8, axis=1)[..., None]
    return vals.transpose(0, 1, 3, 2).reshape(g * 512, n)
def pack4(w):
    words, scales = pack_weight(w, "e2m1")
    return words.reshape(words.shape[0], 128, -1), scales


def unpack4(words, scales):
    return unpack_weight(words.reshape(words.shape[0], 128, -1, 2), scales, "e2m1")


B, N, HID, ITERS = 512, 32, 2048, 10
DOUT = N * N
SLOPE = 0.01
EPS = 1e-8


def leaky(v):
    return np.where(v >= 0.0, v, SLOPE * v)


def l1_normalize(r, axis):
    return r / np.maximum(np.abs(r).sum(axis=axis, keepdims=True), EPS)


def draw0():
    s, t = mx_kscale(HID), mx_kscale(HID)
    h3 = bf(leaky(np.random.standard_normal((B, HID)) * 1.1) * s)
    W4_words, W4_scales = pack4(np.random.standard_normal((HID, HID)) * 1.4 / np.sqrt(HID) / s[:, None] * t)
    b4 = bf(np.random.standard_normal(HID) * 0.3 * t)
    W5_words, W5_scales = pack4(np.random.standard_normal((HID, DOUT)) * 2.0 / np.sqrt(HID) / t[:, None])
    b5 = bf(np.random.standard_normal(DOUT) * 3.0 - 4.0)
    return {"h3": h3,
            "W4_words": W4_words,
            "W4_scales": W4_scales,
            "b4": b4,
            "W5_words": W5_words,
            "W5_scales": W5_scales,
            "b5": b5}


def core(h3, W4_words, W4_scales, b4, W5_words, W5_scales, b5):
    h4 = leaky((mxq(f64(h3), 1, "e4m3") @ unpack4(W4_words, W4_scales)) + f64(b4))
    r = ((mxq(h4, 1, "e4m3") @ unpack4(W5_words, W5_scales)) + f64(b5)).reshape(B, N, N)
    r = np.logaddexp(r, 0.0)
    for _ in range(ITERS):
        r = l1_normalize(r, 1)
        r = l1_normalize(r, 2)
    return r


def e4m3fn_bytes(y):
    return np.clip(np.asarray(y, np.float64), -448.0, 448.0).astype(np.float32).astype(ml_dtypes.float8_e4m3fn).view(np.uint8)


def e4m3fn_values(b):
    return np.asarray(b, np.uint8).view(ml_dtypes.float8_e4m3fn).astype(np.float64)


def setup_inputs():
    d = draw0()
    x0 = np.asarray(d['h3']).astype(np.float64)
    s = (np.max(np.abs(x0), axis=(0,), keepdims=True) / 448.0).astype(np.float32)
    out = {}
    for k, v in d.items():
        if k == 'h3':
            out['h3_bytes'] = e4m3fn_bytes(x0 / s.astype(np.float64))
            out['h3_scale'] = s
        else:
            out[k] = v
    return out


def reference(h3_bytes, h3_scale, W4_words, W4_scales, b4, W5_words, W5_scales, b5):
    return core(e4m3fn_values(h3_bytes) * h3_scale.astype(np.float64), W4_words, W4_scales, b4, W5_words, W5_scales, b5)

@@ -1,0 +1,257 @@
+from contextlib import ExitStack
+
+import concourse.mybir as mybir
+from concourse.masks import make_identity
+
+F32 = mybir.dt.float32
+BF16 = mybir.dt.bfloat16
+I32 = mybir.dt.int32
+U32 = mybir.dt.uint32
+U8 = mybir.dt.uint8
+E4M3 = mybir.dt.float8_e4m3fn
+FP8X4 = mybir.dt.float8_e4m3fn_x4
+FP4X4 = mybir.dt.float4_e2m1fn_x4
+ALU = mybir.AluOpType
+ACTF = mybir.ActivationFunctionType
+AX = mybir.AxisListType
+
+P = 128
+B, HID, DOUT, N, ITERS = 512, 2048, 1024, 32, 10
+SLOPE, EPS, FLOOR = 0.01, 1e-8, 1e-30
+GROUPS = HID // 512
+TILES = B // P
+FLOPS = 2 * B * HID * HID + 2 * B * HID * DOUT
+
+
+def tile_matchingnet_pa_w4_kernel(tc, h3_bytes, h3_scale, W4_words, W4_scales, b4, W5_words, W5_scales, b5, out):
+    nc = tc.nc
+    out2 = out.rearrange("b i j -> b (i j)")
+    with ExitStack() as ctx:
+        keep = ctx.enter_context(tc.tile_pool(name="keep", bufs=1))
+        work = ctx.enter_context(tc.tile_pool(name="work", bufs=2))
+        psum = ctx.enter_context(tc.psum_pool(name="psum", bufs=8))
+
+        def bank(shape, name):
+            return psum.tile(shape, F32, tag="bank", name=name)
+
+        ident = keep.tile([P, P], F32, name="ident")
+        make_identity(nc, ident[:])
+        fold = keep.tile([P, N], F32, name="fold")
+        nc.vector.tensor_reduce(out=fold[:], in_=ident[:].rearrange("p (q j) -> p j q", q=4), axis=AX.X, op=ALU.add)
+
+        w4s = keep.tile([P, GROUPS, HID], U8, name="w4s", align_bytes=64)
+        w5s = keep.tile([P, GROUPS, DOUT], U8, name="w5s", align_bytes=64)
+        w4 = keep.tile([P, GROUPS, 2 * HID], U8, name="w4", align_bytes=64)
+        w5 = keep.tile([P, GROUPS, 2 * DOUT], U8, name="w5", align_bytes=64)
+        b4_t = keep.tile([P, HID], BF16, name="b4_t")
+        b5_t = keep.tile([P, DOUT], BF16, name="b5_t")
+        sc = keep.tile([P, GROUPS, 4], F32, name="sc")
+        x_bytes = [keep.tile([P, HID], U8, name="x_bytes%d" % x, align_bytes=64) for x in range(TILES)]
+
+        nc.vector.memset(w4s[:].rearrange("p g n -> p (g n)").bitcast(I32), 0)
+        nc.vector.memset(w5s[:].rearrange("p g n -> p (g n)").bitcast(I32), 0)
+
+        def load_x(x):
+            nc.sync.dma_start(out=x_bytes[x][:], in_=h3_bytes[x * P:(x + 1) * P, :])
+
+        def load_scales(dst, src):
+            for q in range(4):
+                nc.sync.dma_start(out=dst[32 * q:32 * q + 4, :, :].bitcast(I32), in_=src[:, 4 * q:4 * q + 4, :].rearrange("g q n -> q g n").bitcast(I32))
+
+        load_x(0)
+        nc.sync.dma_start(out=sc[:], in_=h3_scale.rearrange("o (g p t) -> p (o g) t", p=P, t=4))
+        load_scales(w4s, W4_scales)
+        for g in range(GROUPS):
+            nc.sync.dma_start(out=w4[:, g, :], in_=W4_words[g])
+        load_x(1)
+        nc.sync.dma_start(out=b4_t[:], in_=b4.partition_broadcast(P))
+        load_x(2)
+        load_x(3)
+        load_scales(w5s, W5_scales)
+        for g in range(GROUPS):
+            nc.sync.dma_start(out=w5[:, g, :], in_=W5_words[g])
+        nc.sync.dma_start(out=b5_t[:], in_=b5.partition_broadcast(P))
+
+        A = [keep.tile([P, DOUT], F32, name="A%d" % x) for x in range(TILES)]
+        AT = [keep.tile([P, DOUT], F32, name="AT%d" % x) for x in range(TILES)]
+
+        def turn(words, g, pair):
+            for u in range(2):
+                nc.tensor.transpose(pair[:, g % 2, u, :], words[:, 256 * g + u:256 * (g + 1):2], ident[:])
+
+        for x in range(TILES):
+            xb = work.tile([P, HID], BF16, name="xb", align_bytes=64)
+            grouped = work.tile([P, GROUPS, P, 4], BF16, name="grouped", align_bytes=64)
+            codes = work.tile([P, GROUPS * P], U32, name="codes", align_bytes=64)
+            scales = work.tile([P, GROUPS * P], U8, name="scales", align_bytes=64)
+            for g in range(GROUPS):
+                nc.scalar.copy(xb[:, 512 * g:512 * (g + 1)], x_bytes[x][:, 512 * g:512 * (g + 1)].bitcast(E4M3))
+            for gp in range(GROUPS // 2):
+                pair = bank([P, 2, 2, P], "pair")
+                for g in (2 * gp, 2 * gp + 1):
+                    turn(xb[:].bitcast(F32), g, pair)
+                for g in (2 * gp, 2 * gp + 1):
+                    nc.vector.tensor_tensor(
+                        out=grouped[:, g, :, :].rearrange("p r (u e) -> p r u e", e=2),
+                        in0=pair[:, g % 2, :, :].rearrange("p u r -> p (u r)").bitcast(BF16).rearrange("p (u r e) -> p r u e", u=2, e=2),
+                        in1=sc[:, g, :].rearrange("p (u e) -> p u e", e=2).unsqueeze(1).to_broadcast([P, P, 2, 2]),
+                        op=ALU.mult)
+            nc.vector.quantize_mx(out=codes[:].bitcast(FP8X4), scales=scales[:], in_=grouped[:].rearrange("p g r t -> p (g r t)"))
+
+            h4 = work.tile([P, HID], BF16, name="h4", align_bytes=64)
+            for c in range(GROUPS):
+                acc = bank([P, 512], "acc")
+                for g in range(GROUPS):
+                    nc.tensor.matmul_mx(
+                        out=acc[:], lhsT=codes[:, P * g:P * (g + 1)].bitcast(FP8X4), lhsT_scale=scales[:, P * g:P * (g + 1)],
+                        rhs=w4[:, g, 1024 * c:1024 * (c + 1)].bitcast(FP4X4), rhs_scale=w4s[:, g, 512 * c:512 * (c + 1)],
+                        start=(g == 0), stop=(g == GROUPS - 1))
+                y = work.tile([P, 512], F32, name="y", bufs=3)
+                nc.vector.tensor_tensor(out=y[:], in0=acc[:], in1=b4_t[:, 512 * c:512 * (c + 1)], op=ALU.add)
+                nc.vector.scalar_tensor_tensor(out=h4[:, 512 * c:512 * (c + 1)], in0=y[:], scalar=SLOPE, in1=y[:], op0=ALU.mult, op1=ALU.max)
+            grouped4 = work.tile([P, GROUPS, P, 4], BF16, name="grouped4", align_bytes=64)
+            codes4 = work.tile([P, GROUPS * P], U32, name="codes4", align_bytes=64)
+            scales4 = work.tile([P, GROUPS * P], U8, name="scales4", align_bytes=64)
+            for gp in range(GROUPS // 2):
+                pair = bank([P, 2, 2, P], "pair4")
+                for g in (2 * gp, 2 * gp + 1):
+                    turn(h4[:].bitcast(F32), g, pair)
+                nc.scalar.copy(
+                    grouped4[:, 2 * gp:2 * gp + 2, :, :].rearrange("p g r t -> p (g r t)").bitcast(F32).rearrange("p (g r u) -> p g r u", g=2, u=2),
+                    pair[:].rearrange("p g u r -> p g r u"))
+            nc.vector.quantize_mx(out=codes4[:].bitcast(FP8X4), scales=scales4[:], in_=grouped4[:].rearrange("p g r t -> p (g r t)"))
+            zs = []
+            for c in range(2):
+                cs = slice(512 * c, 512 * (c + 1))
+                acc = bank([P, 512], "acc2")
+                for g in range(GROUPS):
+                    nc.tensor.matmul_mx(
+                        out=acc[:], lhsT=codes4[:, P * g:P * (g + 1)].bitcast(FP8X4), lhsT_scale=scales4[:, P * g:P * (g + 1)],
+                        rhs=w5[:, g, 1024 * c:1024 * (c + 1)].bitcast(FP4X4), rhs_scale=w5s[:, g, cs],
+                        start=(g == 0), stop=(g == GROUPS - 1))
+                z = work.tile([P, 512], F32, name="z", bufs=8)
+                n = work.tile([P, 512], F32, name="n", bufs=8)
+                nc.vector.tensor_tensor(out=z[:], in0=acc[:], in1=b5_t[:, cs], op=ALU.add)
+                nc.scalar.activation(n[:], z[:], ACTF.Abs)
+                nc.scalar.activation(n[:], n[:], ACTF.Exp, scale=-1.0)
+                zs.append((z, n))
+            for c in range(2):
+                z, n = zs[c]
+                nc.scalar.activation(n[:], n[:], ACTF.Ln, bias=1.0)
+                nc.vector.scalar_tensor_tensor(out=A[x][:, 512 * c:512 * (c + 1)], in0=z[:], scalar=FLOOR, in1=n[:], op0=ALU.max, op1=ALU.add)
+            nc.scalar.copy(AT[x][:].rearrange("p (a c i) -> p a i c", a=8, c=4), A[x][:].rearrange("p (i a c) -> p a i c", a=8, c=4))
+
+        slots = 2 * ITERS * TILES
+        EXACT = slots - 2 * TILES
+        VEC_ROWS = 22
+        SPLIT = 12
+        prod, turned, sums, inv, y_of, part = {}, {}, {}, {}, {}, {}
+
+        def source(n):
+            h, x = divmod(n, TILES)
+            return A[x] if h % 2 == 0 else AT[x]
+
+        def vec_rows(n, r0, r1):
+            cols = slice(N * r0, N * r1)
+            nc.vector.tensor_tensor(
+                out=prod[n][:, cols].rearrange("p (a c) -> p a c", c=N), in0=source(n)[:, cols].rearrange("p (a c) -> p a c", c=N),
+                in1=inv[n - TILES][:, r0:r1].unsqueeze(2).to_broadcast([P, r1 - r0, N]), op=ALU.mult)
+
+        def act_rows(n, r0, r1):
+            for a in range(r0, r1):
+                cols = slice(N * a, N * (a + 1))
+                nc.scalar.activation(prod[n][:, cols], source(n)[:, cols], ACTF.Copy, scale=inv[n - TILES][:, a:a + 1])
+
+        def turn_chunks(n, ks, first, last):
+            for k in ks:
+                nc.tensor.matmul(out=turned[n][:], lhsT=prod[n][:, P * k:P * (k + 1)], rhs=ident[:], is_transpose=True, start=(k == first), stop=(k == last))
+
+        def take_turned(n):
+            ts = work.tile([P, P], F32, name="ts", bufs=4)
+            nc.scalar.copy(ts[:], turned[n][:])
+            sums[n] = bank([P, N], "sums")
+            nc.tensor.matmul(out=sums[n][:], lhsT=ts[:], rhs=fold[:], start=True, stop=True)
+
+        def clamp(n):
+            yn = work.tile([P, N], F32, name="yn", bufs=16)
+            if n < 2 * TILES:
+                nc.vector.tensor_scalar(out=yn[:], in0=sums[n][:], scalar1=EPS, scalar2=None, op0=ALU.max)
+            else:
+                nc.vector.scalar_tensor_tensor(out=yn[:], in0=y_of[n - 2 * TILES][:], scalar=EPS, in1=sums[n][:], op0=ALU.mult, op1=ALU.max)
+            y_of[n] = yn
+
+        def root(n):
+            w = work.tile([P, N], F32, name="w", bufs=16)
+            inv[n] = w
+            q = work.tile([P, N], F32, name="q", bufs=4)
+            part[n] = q
+            nc.scalar.activation(q[:], y_of[n][:], ACTF.Abs_reciprocal_sqrt)
+
+        def square(n):
+            nc.scalar.activation(inv[n][:], part[n][:], ACTF.Square)
+
+        def exact(n):
+            w = work.tile([P, N], F32, name="w", bufs=16)
+            inv[n] = w
+            nc.vector.reciprocal(w[:], y_of[n][:])
+
+        rows_t = {}
+
+        def row_scaled(x):
+            v = inv[(2 * ITERS - 2) * TILES + x]
+            r = work.tile([P, DOUT], F32, name="r", bufs=4)
+            rows_t[x] = r
+            nc.vector.tensor_tensor(out=r[:].rearrange("p (i j) -> p i j", j=N), in0=A[x][:].rearrange("p (i j) -> p i j", j=N), in1=v[:].unsqueeze(1).to_broadcast([P, N, N]), op=ALU.mult)
+
+        def finish(x):
+            u = inv[(2 * ITERS - 1) * TILES + x]
+            r = rows_t[x]
+            o = work.tile([P, DOUT], F32, name="o", bufs=2)
+            cut = 18
+            nc.vector.tensor_tensor(out=o[:, 0:N * cut].rearrange("p (i j) -> p i j", j=N), in0=r[:, 0:N * cut].rearrange("p (i j) -> p i j", j=N), in1=u[:, 0:cut].unsqueeze(2).to_broadcast([P, cut, N]), op=ALU.mult)
+            for a in range(cut, N):
+                cols = slice(N * a, N * (a + 1))
+                nc.scalar.activation(o[:, cols], r[:, cols], ACTF.Copy, scale=u[:, a:a + 1])
+            nc.sync.dma_start(out=out2[x * P:(x + 1) * P, :], in_=o[:])
+
+        with tc.manual_schedule():
+            for n in range(slots + 2):
+                live = n < slots
+                full = live and n >= TILES
+                if live:
+                    turned[n] = bank([P, P], "turned")
+                if full:
+                    prod[n] = work.tile([P, DOUT], F32, name="prod", bufs=4)
+                    vec_rows(n, 0, SPLIT)
+                    act_rows(n, 24, 28)
+                    turn_chunks(n, (6, 0, 1, 2), 6, 5)
+                elif live:
+                    prod[n] = A[n]
+                    turn_chunks(n, (6, 0, 1, 2), 6, 5)
+                if 1 <= n <= slots:
+                    take_turned(n - 1)
+                if full:
+                    act_rows(n, 28, 32)
+                if live:
+                    turn_chunks(n, (7,), 6, 5)
+                if n >= 2:
+                    clamp(n - 2)
+                if full:
+                    vec_rows(n, SPLIT, VEC_ROWS)
+                if live:
+                    turn_chunks(n, (3, 4), 6, 5)
+                if n >= 2:
+                    if n - 2 < EXACT:
+                        root(n - 2)
+                    else:
+                        exact(n - 2)
+                if full:
+                    act_rows(n, VEC_ROWS, 24)
+                if live:
+                    turn_chunks(n, (5,), 6, 5)
+                if 2 <= n and n - 2 < EXACT:
+                    square(n - 2)
+                if live and n >= slots - TILES:
+                    row_scaled(n % TILES)
+                if n - 2 >= slots - TILES:
+                    finish((n - 2) % TILES)

@@ -18,6 +18,7 @@ AX = mybir.AxisListType
 P = 128
 B, HID, DOUT, N, ITERS = 512, 2048, 1024, 32, 10
 SLOPE, EPS, FLOOR = 0.01, 1e-8, 1e-30
+FOLD = 32
 GROUPS = HID // 512
 TILES = B // P
 FLOPS = 2 * B * HID * HID + 2 * B * HID * DOUT
@@ -36,20 +37,18 @@ def tile_matchingnet_pa_w4_kernel(tc, h3_bytes, h3_scale, W4_words, W4_scales, b
 
         ident = keep.tile([P, P], F32, name="ident")
         make_identity(nc, ident[:])
-        fold = keep.tile([P, N], F32, name="fold")
-        nc.vector.tensor_reduce(out=fold[:], in_=ident[:].rearrange("p (q j) -> p j q", q=4), axis=AX.X, op=ALU.add)
+        fold = keep.tile([P, FOLD], F32, name="fold")
 
         w4s = keep.tile([P, GROUPS, HID], U8, name="w4s", align_bytes=64)
         w5s = keep.tile([P, GROUPS, DOUT], U8, name="w5s", align_bytes=64)
-        w4 = keep.tile([P, GROUPS, 2 * HID], U8, name="w4", align_bytes=64)
-        w5 = keep.tile([P, GROUPS, 2 * DOUT], U8, name="w5", align_bytes=64)
+        w4 = [keep.tile([P, GROUPS, 1024], U8, name="w4_%d" % c, align_bytes=64) for c in range(4)]
+        w5 = [keep.tile([P, GROUPS, 1024], U8, name="w5_%d" % c, align_bytes=64) for c in range(2)]
         b4_t = keep.tile([P, HID], BF16, name="b4_t")
         b5_t = keep.tile([P, DOUT], BF16, name="b5_t")
         sc = keep.tile([P, GROUPS, 4], F32, name="sc")
         x_bytes = [keep.tile([P, HID], U8, name="x_bytes%d" % x, align_bytes=64) for x in range(TILES)]
 
-        nc.vector.memset(w4s[:].rearrange("p g n -> p (g n)").bitcast(I32), 0)
-        nc.vector.memset(w5s[:].rearrange("p g n -> p (g n)").bitcast(I32), 0)
+        nc.gpsimd.memset(w5s[:].rearrange("p g n -> p (g n)").bitcast(I32), 0)
 
         def load_x(x):
             nc.sync.dma_start(out=x_bytes[x][:], in_=h3_bytes[x * P:(x + 1) * P, :])
@@ -58,150 +57,178 @@ def tile_matchingnet_pa_w4_kernel(tc, h3_bytes, h3_scale, W4_words, W4_scales, b
             for q in range(4):
                 nc.sync.dma_start(out=dst[32 * q:32 * q + 4, :, :].bitcast(I32), in_=src[:, 4 * q:4 * q + 4, :].rearrange("g q n -> q g n").bitcast(I32))
 
+        ctx.enter_context(tc.manual_schedule())
+        warm = keep.tile([P, 1], F32, name="warm")
+        nc.vector.memset(warm[:], 1.0)
+        nc.scalar.activation(warm[:], warm[:], ACTF.Exp)
+        nc.vector.memset(w4s[:].rearrange("p g n -> p (g n)").bitcast(I32), 0)
         load_x(0)
         nc.sync.dma_start(out=sc[:], in_=h3_scale.rearrange("o (g p t) -> p (o g) t", p=P, t=4))
-        load_scales(w4s, W4_scales)
-        for g in range(GROUPS):
-            nc.sync.dma_start(out=w4[:, g, :], in_=W4_words[g])
         load_x(1)
-        nc.sync.dma_start(out=b4_t[:], in_=b4.partition_broadcast(P))
+        load_scales(w4s, W4_scales)
+
+        def load_words(dst, src, c):
+            nc.sync.dma_start(out=dst[c][:], in_=src[:, :, 1024 * c:1024 * (c + 1)].rearrange("g p n -> p g n"))
+
+        def load_bias(dst, src, c0, c1):
+            nc.sync.dma_start(out=dst[:, c0:c1], in_=src[c0:c1].partition_broadcast(P))
+
+        load_words(w4, W4_words, 0)
+        load_bias(b4_t, b4, 0, 1024)
+        load_words(w4, W4_words, 1)
+        load_words(w4, W4_words, 2)
+        load_bias(b4_t, b4, 1024, 2048)
+        load_words(w4, W4_words, 3)
         load_x(2)
-        load_x(3)
         load_scales(w5s, W5_scales)
-        for g in range(GROUPS):
-            nc.sync.dma_start(out=w5[:, g, :], in_=W5_words[g])
-        nc.sync.dma_start(out=b5_t[:], in_=b5.partition_broadcast(P))
+        load_words(w5, W5_words, 0)
+        load_words(w5, W5_words, 1)
+        load_x(3)
+        load_bias(b5_t, b5, 0, DOUT)
 
         A = [keep.tile([P, DOUT], F32, name="A%d" % x) for x in range(TILES)]
         AT = [keep.tile([P, DOUT], F32, name="AT%d" % x) for x in range(TILES)]
+
+        xb, grouped, codes, scales, pairs, h4, grouped4, codes4, scales4, accs, ys, zs, ns = {}, {}, {}, {}, {}, {}, {}, {}, {}, {}, {}, {}, {}
 
         def turn(words, g, pair):
             for u in range(2):
                 nc.tensor.transpose(pair[:, g % 2, u, :], words[:, 256 * g + u:256 * (g + 1):2], ident[:])
 
-        for x in range(TILES):
-            xb = work.tile([P, HID], BF16, name="xb", align_bytes=64)
-            grouped = work.tile([P, GROUPS, P, 4], BF16, name="grouped", align_bytes=64)
-            codes = work.tile([P, GROUPS * P], U32, name="codes", align_bytes=64)
-            scales = work.tile([P, GROUPS * P], U8, name="scales", align_bytes=64)
-            for g in range(GROUPS):
-                nc.scalar.copy(xb[:, 512 * g:512 * (g + 1)], x_bytes[x][:, 512 * g:512 * (g + 1)].bitcast(E4M3))
-            for gp in range(GROUPS // 2):
-                pair = bank([P, 2, 2, P], "pair")
-                for g in (2 * gp, 2 * gp + 1):
-                    turn(xb[:].bitcast(F32), g, pair)
-                for g in (2 * gp, 2 * gp + 1):
-                    nc.vector.tensor_tensor(
-                        out=grouped[:, g, :, :].rearrange("p r (u e) -> p r u e", e=2),
-                        in0=pair[:, g % 2, :, :].rearrange("p u r -> p (u r)").bitcast(BF16).rearrange("p (u r e) -> p r u e", u=2, e=2),
-                        in1=sc[:, g, :].rearrange("p (u e) -> p u e", e=2).unsqueeze(1).to_broadcast([P, P, 2, 2]),
-                        op=ALU.mult)
-            nc.vector.quantize_mx(out=codes[:].bitcast(FP8X4), scales=scales[:], in_=grouped[:].rearrange("p g r t -> p (g r t)"))
+        def widen(x, g, on_vector=False):
+            if g == 0:
+                xb[x] = work.tile([P, HID], BF16, name="xb", align_bytes=64)
+            dst, src = xb[x][:, 512 * g:512 * (g + 1)], x_bytes[x][:, 512 * g:512 * (g + 1)].bitcast(E4M3)
+            if on_vector:
+                nc.vector.tensor_copy(out=dst, in_=src)
+            else:
+                nc.scalar.copy(dst, src)
 
-            h4 = work.tile([P, HID], BF16, name="h4", align_bytes=64)
-            for c in range(GROUPS):
-                acc = bank([P, 512], "acc")
-                for g in range(GROUPS):
-                    nc.tensor.matmul_mx(
-                        out=acc[:], lhsT=codes[:, P * g:P * (g + 1)].bitcast(FP8X4), lhsT_scale=scales[:, P * g:P * (g + 1)],
-                        rhs=w4[:, g, 1024 * c:1024 * (c + 1)].bitcast(FP4X4), rhs_scale=w4s[:, g, 512 * c:512 * (c + 1)],
-                        start=(g == 0), stop=(g == GROUPS - 1))
-                y = work.tile([P, 512], F32, name="y", bufs=3)
-                nc.vector.tensor_tensor(out=y[:], in0=acc[:], in1=b4_t[:, 512 * c:512 * (c + 1)], op=ALU.add)
-                nc.vector.scalar_tensor_tensor(out=h4[:, 512 * c:512 * (c + 1)], in0=y[:], scalar=SLOPE, in1=y[:], op0=ALU.mult, op1=ALU.max)
-            grouped4 = work.tile([P, GROUPS, P, 4], BF16, name="grouped4", align_bytes=64)
-            codes4 = work.tile([P, GROUPS * P], U32, name="codes4", align_bytes=64)
-            scales4 = work.tile([P, GROUPS * P], U8, name="scales4", align_bytes=64)
-            for gp in range(GROUPS // 2):
-                pair = bank([P, 2, 2, P], "pair4")
-                for g in (2 * gp, 2 * gp + 1):
-                    turn(h4[:].bitcast(F32), g, pair)
-                nc.scalar.copy(
-                    grouped4[:, 2 * gp:2 * gp + 2, :, :].rearrange("p g r t -> p (g r t)").bitcast(F32).rearrange("p (g r u) -> p g r u", g=2, u=2),
-                    pair[:].rearrange("p g u r -> p g r u"))
-            nc.vector.quantize_mx(out=codes4[:].bitcast(FP8X4), scales=scales4[:], in_=grouped4[:].rearrange("p g r t -> p (g r t)"))
-            zs = []
+        def turn_x(x, gp):
+            pairs[x, gp] = bank([P, 2, 2, P], "pair")
+            for g in (2 * gp, 2 * gp + 1):
+                turn(xb[x][:].bitcast(F32), g, pairs[x, gp])
+
+        def scale_x(x, g):
+            if g == 0:
+                grouped[x] = work.tile([P, GROUPS, P, 4], BF16, name="grouped", align_bytes=64)
+            nc.vector.tensor_tensor(
+                out=grouped[x][:, g, :, :].rearrange("p r (u e) -> p r u e", e=2),
+                in0=pairs[x, g // 2][:, g % 2, :, :].rearrange("p u r -> p (u r)").bitcast(BF16).rearrange("p (u r e) -> p r u e", u=2, e=2),
+                in1=sc[:, g, :].rearrange("p (u e) -> p u e", e=2).unsqueeze(1).to_broadcast([P, P, 2, 2]),
+                op=ALU.mult)
+
+        def quant_x(x, g0=0, g1=GROUPS):
+            if g0 == 0:
+                codes[x] = work.tile([P, GROUPS * P], U32, name="codes", align_bytes=64)
+                scales[x] = work.tile([P, GROUPS * P], U8, name="scales", align_bytes=64)
+            cols = slice(P * g0, P * g1)
+            nc.vector.quantize_mx(out=codes[x][:, cols].bitcast(FP8X4), scales=scales[x][:, cols], in_=grouped[x][:, g0:g1, :, :].rearrange("p g r t -> p (g r t)"))
+
+        def layer(acc, c, cw, sw, w, ws):
+            for g in range(GROUPS):
+                nc.tensor.matmul_mx(
+                    out=acc[:], lhsT=cw[:, P * g:P * (g + 1)].bitcast(FP8X4), lhsT_scale=sw[:, P * g:P * (g + 1)],
+                    rhs=w[c][:, g, :].bitcast(FP4X4), rhs_scale=ws[:, g, 512 * c:512 * (c + 1)],
+                    start=(g == 0), stop=(g == GROUPS - 1))
+
+        def layer4(x, c):
+            accs[x, c] = bank([P, 512], "acc")
+            layer(accs[x, c], c, codes[x], scales[x], w4, w4s)
+
+        def bias4(x, c):
+            ys[x, c] = work.tile([P, 512], F32, name="y", bufs=3)
+            nc.vector.tensor_tensor(out=ys[x, c][:], in0=accs[x, c][:], in1=b4_t[:, 512 * c:512 * (c + 1)], op=ALU.add)
+
+        def leak4(x, c):
+            if c == 0:
+                h4[x] = work.tile([P, HID], BF16, name="h4", align_bytes=64)
+            y = ys[x, c]
+            nc.vector.scalar_tensor_tensor(out=h4[x][:, 512 * c:512 * (c + 1)], in0=y[:], scalar=SLOPE, in1=y[:], op0=ALU.mult, op1=ALU.max)
+
+        def turn_h(x, gp):
+            pair = bank([P, 2, 2, P], "pair4")
+            for g in (2 * gp, 2 * gp + 1):
+                turn(h4[x][:].bitcast(F32), g, pair)
+            if gp == 0:
+                grouped4[x] = work.tile([P, GROUPS, P, 4], BF16, name="grouped4", align_bytes=64)
+            nc.scalar.copy(
+                grouped4[x][:, 2 * gp:2 * gp + 2, :, :].rearrange("p g r t -> p (g r t)").bitcast(F32).rearrange("p (g r u) -> p g r u", g=2, u=2),
+                pair[:].rearrange("p g u r -> p g r u"))
+
+        def quant_h(x, g0=0, g1=GROUPS):
+            if g0 == 0:
+                codes4[x] = work.tile([P, GROUPS * P], U32, name="codes4", align_bytes=64)
+                scales4[x] = work.tile([P, GROUPS * P], U8, name="scales4", align_bytes=64)
+            cols = slice(P * g0, P * g1)
+            nc.vector.quantize_mx(out=codes4[x][:, cols].bitcast(FP8X4), scales=scales4[x][:, cols], in_=grouped4[x][:, g0:g1, :, :].rearrange("p g r t -> p (g r t)"))
+
+        def layer5(x, c):
+            accs[x, c] = bank([P, 512], "acc2")
+            layer(accs[x, c], c, codes4[x], scales4[x], w5, w5s)
+
+        def bias5(x, c):
+            zs[x, c] = work.tile([P, 512], F32, name="z", bufs=8)
+            ns[x, c] = work.tile([P, 512], F32, name="n", bufs=8)
+            nc.vector.tensor_tensor(out=zs[x, c][:], in0=accs[x, c][:], in1=b5_t[:, 512 * c:512 * (c + 1)], op=ALU.add)
+            nc.scalar.activation(ns[x, c][:], zs[x, c][:], ACTF.Abs)
+            nc.scalar.activation(ns[x, c][:], ns[x, c][:], ACTF.Exp, scale=-1.0)
+
+        def log5(x):
             for c in range(2):
-                cs = slice(512 * c, 512 * (c + 1))
-                acc = bank([P, 512], "acc2")
-                for g in range(GROUPS):
-                    nc.tensor.matmul_mx(
-                        out=acc[:], lhsT=codes4[:, P * g:P * (g + 1)].bitcast(FP8X4), lhsT_scale=scales4[:, P * g:P * (g + 1)],
-                        rhs=w5[:, g, 1024 * c:1024 * (c + 1)].bitcast(FP4X4), rhs_scale=w5s[:, g, cs],
-                        start=(g == 0), stop=(g == GROUPS - 1))
-                z = work.tile([P, 512], F32, name="z", bufs=8)
-                n = work.tile([P, 512], F32, name="n", bufs=8)
-                nc.vector.tensor_tensor(out=z[:], in0=acc[:], in1=b5_t[:, cs], op=ALU.add)
-                nc.scalar.activation(n[:], z[:], ACTF.Abs)
-                nc.scalar.activation(n[:], n[:], ACTF.Exp, scale=-1.0)
-                zs.append((z, n))
+                nc.scalar.activation(ns[x, c][:], ns[x, c][:], ACTF.Ln, bias=1.0)
+
+        def soft5(x):
             for c in range(2):
-                z, n = zs[c]
-                nc.scalar.activation(n[:], n[:], ACTF.Ln, bias=1.0)
-                nc.vector.scalar_tensor_tensor(out=A[x][:, 512 * c:512 * (c + 1)], in0=z[:], scalar=FLOOR, in1=n[:], op0=ALU.max, op1=ALU.add)
+                nc.vector.scalar_tensor_tensor(out=A[x][:, 512 * c:512 * (c + 1)], in0=zs[x, c][:], scalar=FLOOR, in1=ns[x, c][:], op0=ALU.max, op1=ALU.add)
             nc.scalar.copy(AT[x][:].rearrange("p (a c i) -> p a i c", a=8, c=4), A[x][:].rearrange("p (i a c) -> p a i c", a=8, c=4))
 
         slots = 2 * ITERS * TILES
-        EXACT = slots - 2 * TILES
-        VEC_ROWS = 22
-        SPLIT = 12
-        prod, turned, sums, inv, y_of, part = {}, {}, {}, {}, {}, {}
+        prod, turned, sums, inv, turned_sb, rows_t = {}, {}, {}, {}, {}, {}
 
         def source(n):
             h, x = divmod(n, TILES)
             return A[x] if h % 2 == 0 else AT[x]
 
-        def vec_rows(n, r0, r1):
+        def scale_vec(n, r0, r1):
             cols = slice(N * r0, N * r1)
             nc.vector.tensor_tensor(
                 out=prod[n][:, cols].rearrange("p (a c) -> p a c", c=N), in0=source(n)[:, cols].rearrange("p (a c) -> p a c", c=N),
                 in1=inv[n - TILES][:, r0:r1].unsqueeze(2).to_broadcast([P, r1 - r0, N]), op=ALU.mult)
 
-        def act_rows(n, r0, r1):
+        def scale_act(n, r0, r1):
             for a in range(r0, r1):
                 cols = slice(N * a, N * (a + 1))
                 nc.scalar.activation(prod[n][:, cols], source(n)[:, cols], ACTF.Copy, scale=inv[n - TILES][:, a:a + 1])
 
-        def turn_chunks(n, ks, first, last):
-            for k in ks:
-                nc.tensor.matmul(out=turned[n][:], lhsT=prod[n][:, P * k:P * (k + 1)], rhs=ident[:], is_transpose=True, start=(k == first), stop=(k == last))
+        def turn_chunk(n, k, first, last):
+            nc.tensor.matmul(out=turned[n][:], lhsT=prod[n][:, P * k:P * (k + 1)], rhs=ident[:], is_transpose=True, start=first, stop=last)
 
-        def take_turned(n):
-            ts = work.tile([P, P], F32, name="ts", bufs=4)
-            nc.scalar.copy(ts[:], turned[n][:])
-            sums[n] = bank([P, N], "sums")
-            nc.tensor.matmul(out=sums[n][:], lhsT=ts[:], rhs=fold[:], start=True, stop=True)
+        def take(n):
+            turned_sb[n] = work.tile([P, P], F32, name="ts", bufs=4)
+            nc.scalar.copy(turned_sb[n][:], turned[n][:])
+
+        def fold_sum(n):
+            sums[n] = bank([P, FOLD], "sums")
+            nc.tensor.matmul(out=sums[n][:], lhsT=turned_sb[n][:], rhs=fold[:], start=True, stop=True)
+
+        raw = {}
+
+        def invert(n):
+            raw[n] = work.tile([P, N], F32, name="raw", bufs=16)
+            nc.vector.reciprocal(raw[n][:], sums[n][:, 0:N])
 
         def clamp(n):
-            yn = work.tile([P, N], F32, name="yn", bufs=16)
+            inv[n] = work.tile([P, N], F32, name="inv", bufs=16)
             if n < 2 * TILES:
-                nc.vector.tensor_scalar(out=yn[:], in0=sums[n][:], scalar1=EPS, scalar2=None, op0=ALU.max)
+                nc.vector.tensor_scalar(out=inv[n][:], in0=raw[n][:], scalar1=1.0 / EPS, scalar2=None, op0=ALU.min)
             else:
-                nc.vector.scalar_tensor_tensor(out=yn[:], in0=y_of[n - 2 * TILES][:], scalar=EPS, in1=sums[n][:], op0=ALU.mult, op1=ALU.max)
-            y_of[n] = yn
-
-        def root(n):
-            w = work.tile([P, N], F32, name="w", bufs=16)
-            inv[n] = w
-            q = work.tile([P, N], F32, name="q", bufs=4)
-            part[n] = q
-            nc.scalar.activation(q[:], y_of[n][:], ACTF.Abs_reciprocal_sqrt)
-
-        def square(n):
-            nc.scalar.activation(inv[n][:], part[n][:], ACTF.Square)
-
-        def exact(n):
-            w = work.tile([P, N], F32, name="w", bufs=16)
-            inv[n] = w
-            nc.vector.reciprocal(w[:], y_of[n][:])
-
-        rows_t = {}
+                nc.vector.scalar_tensor_tensor(out=inv[n][:], in0=inv[n - 2 * TILES][:], scalar=1.0 / EPS, in1=raw[n][:], op0=ALU.mult, op1=ALU.min)
 
         def row_scaled(x):
             v = inv[(2 * ITERS - 2) * TILES + x]
-            r = work.tile([P, DOUT], F32, name="r", bufs=4)
-            rows_t[x] = r
-            nc.vector.tensor_tensor(out=r[:].rearrange("p (i j) -> p i j", j=N), in0=A[x][:].rearrange("p (i j) -> p i j", j=N), in1=v[:].unsqueeze(1).to_broadcast([P, N, N]), op=ALU.mult)
+            rows_t[x] = work.tile([P, DOUT], F32, name="r", bufs=4)
+            nc.vector.tensor_tensor(out=rows_t[x][:].rearrange("p (i j) -> p i j", j=N), in0=A[x][:].rearrange("p (i j) -> p i j", j=N), in1=v[:].unsqueeze(1).to_broadcast([P, N, N]), op=ALU.mult)
 
         def finish(x):
             u = inv[(2 * ITERS - 1) * TILES + x]
@@ -214,44 +241,130 @@ def tile_matchingnet_pa_w4_kernel(tc, h3_bytes, h3_scale, W4_words, W4_scales, b
                 nc.scalar.activation(o[:, cols], r[:, cols], ACTF.Copy, scale=u[:, a:a + 1])
             nc.sync.dma_start(out=out2[x * P:(x + 1) * P, :], in_=o[:])
 
-        with tc.manual_schedule():
-            for n in range(slots + 2):
-                live = n < slots
-                full = live and n >= TILES
-                if live:
-                    turned[n] = bank([P, P], "turned")
-                if full:
-                    prod[n] = work.tile([P, DOUT], F32, name="prod", bufs=4)
-                    vec_rows(n, 0, SPLIT)
-                    act_rows(n, 24, 28)
-                    turn_chunks(n, (6, 0, 1, 2), 6, 5)
-                elif live:
-                    prod[n] = A[n]
-                    turn_chunks(n, (6, 0, 1, 2), 6, 5)
-                if 1 <= n <= slots:
-                    take_turned(n - 1)
-                if full:
-                    act_rows(n, 28, 32)
-                if live:
-                    turn_chunks(n, (7,), 6, 5)
-                if n >= 2:
-                    clamp(n - 2)
-                if full:
-                    vec_rows(n, SPLIT, VEC_ROWS)
-                if live:
-                    turn_chunks(n, (3, 4), 6, 5)
-                if n >= 2:
-                    if n - 2 < EXACT:
-                        root(n - 2)
-                    else:
-                        exact(n - 2)
-                if full:
-                    act_rows(n, VEC_ROWS, 24)
-                if live:
-                    turn_chunks(n, (5,), 6, 5)
-                if 2 <= n and n - 2 < EXACT:
-                    square(n - 2)
-                if live and n >= slots - TILES:
-                    row_scaled(n % TILES)
-                if n - 2 >= slots - TILES:
-                    finish((n - 2) % TILES)
+        def slot(n):
+            live, full = n < slots, TILES <= n < slots
+            if live:
+                turned[n] = bank([P, P], "turned")
+                prod[n] = work.tile([P, DOUT], F32, name="prod", bufs=4) if full else A[n]
+            if full:
+                scale_vec(n, 0, 12)
+            if full:
+                scale_act(n, 20, 24)
+            if 0 <= n - 3 < slots:
+                clamp(n - 3)
+            if full:
+                scale_act(n, 24, 28)
+            if live:
+                turn_chunk(n, 6, True, False)
+            if live:
+                turn_chunk(n, 5, False, False)
+            if live:
+                turn_chunk(n, 1, False, False)
+            if live:
+                turn_chunk(n, 0, False, False)
+            if live:
+                turn_chunk(n, 2, False, False)
+            if full:
+                scale_vec(n, 12, 17)
+            if live:
+                turn_chunk(n, 3, False, False)
+            if full:
+                scale_act(n, 28, 32)
+            if 0 <= n - 2 < slots:
+                invert(n - 2)
+            if full:
+                scale_act(n, 17, 20)
+            if live:
+                turn_chunk(n, 4, False, False)
+            if live:
+                turn_chunk(n, 7, False, True)
+            if 0 <= n - 1 < slots:
+                take(n - 1)
+            if 0 <= n - 1 < slots:
+                fold_sum(n - 1)
+            if live and n >= slots - TILES:
+                row_scaled(n % TILES)
+            if n - 3 >= slots - TILES:
+                finish((n - 3) % TILES)
+
+        for i in range(FOLD // N):
+            nc.vector.tensor_reduce(out=fold[:, N * i:N * (i + 1)], in_=ident[:].rearrange("p (q j) -> p j q", q=4), axis=AX.X, op=ALU.add)
+        for g in range(GROUPS):
+            widen(0, g, g % 2 == 1)
+        turn_x(0, 0)
+        turn_x(0, 1)
+        for g in range(GROUPS):
+            widen(1, g)
+        for g in range(GROUPS):
+            scale_x(0, g)
+        quant_x(0, 0, 2)
+        turn_x(1, 0)
+        quant_x(0, 2, 4)
+        turn_x(1, 1)
+        for g in range(GROUPS):
+            scale_x(1, g)
+        quant_x(1)
+        for x in range(TILES):
+            ahead = x + 1 if 0 < x < TILES - 1 else 0
+            layer4(x, 0)
+            bias4(x, 0)
+            layer4(x, 1)
+            if x > 0:
+                turn_h(x - 1, 1)
+            if ahead:
+                turn_x(ahead, 0)
+                turn_x(ahead, 1)
+                scale_x(ahead, 0)
+            leak4(x, 0)
+            bias4(x, 1)
+            if ahead:
+                scale_x(ahead, 1)
+            if x > 0:
+                quant_h(x - 1)
+            leak4(x, 1)
+            if x == 3:
+                log5(0)
+                log5(1)
+                soft5(0)
+            layer4(x, 2)
+            if x > 0:
+                layer5(x - 1, 0)
+            bias4(x, 2)
+            if ahead:
+                scale_x(ahead, 2)
+            leak4(x, 2)
+            if x == 3:
+                soft5(1)
+            if x > 0:
+                bias5(x - 1, 0)
+            layer4(x, 3)
+            if x > 0:
+                layer5(x - 1, 1)
+            turn_h(x, 0)
+            if ahead:
+                scale_x(ahead, 3)
+            bias4(x, 3)
+            if ahead:
+                quant_x(ahead)
+            leak4(x, 3)
+            if x > 0:
+                bias5(x - 1, 1)
+            if 0 <= x < 2:
+                for g in range(GROUPS):
+                    widen(x + 2, g)
+        turn_h(3, 1)
+        quant_h(3, 0, 2)
+        quant_h(3, 2, 4)
+        layer5(3, 0)
+        layer5(3, 1)
+        bias5(3, 0)
+        bias5(3, 1)
+        slot(0)
+        slot(1)
+        log5(2)
+        soft5(2)
+        slot(2)
+        log5(3)
+        soft5(3)
+        for n in range(3, slots + 4):
+            slot(n)

@@ -18,7 +18,7 @@ AX = mybir.AxisListType
 P = 128
 B, HID, DOUT, N, ITERS = 512, 2048, 1024, 32, 10
 SLOPE, EPS, FLOOR = 0.01, 1e-8, 1e-30
-FOLD = 32
+FOLD = 160
 GROUPS = HID // 512
 TILES = B // P
 FLOPS = 2 * B * HID * HID + 2 * B * HID * DOUT
@@ -91,9 +91,10 @@ def tile_matchingnet_pa_w4_kernel(tc, h3_bytes, h3_scale, W4_words, W4_scales, b
 
         xb, grouped, codes, scales, pairs, h4, grouped4, codes4, scales4, accs, ys, zs, ns = {}, {}, {}, {}, {}, {}, {}, {}, {}, {}, {}, {}, {}
 
-        def turn(words, g, pair):
+        def turn(words, g, pair, apart):
             for u in range(2):
-                nc.tensor.transpose(pair[:, g % 2, u, :], words[:, 256 * g + u:256 * (g + 1):2], ident[:])
+                cols = slice(256 * g + 128 * u, 256 * g + 128 * (u + 1)) if apart else slice(256 * g + u, 256 * (g + 1), 2)
+                nc.tensor.transpose(pair[:, g % 2, u, :], words[:, cols], ident[:])
 
         def widen(x, g, on_vector=False):
             if g == 0:
@@ -107,7 +108,7 @@ def tile_matchingnet_pa_w4_kernel(tc, h3_bytes, h3_scale, W4_words, W4_scales, b
         def turn_x(x, gp):
             pairs[x, gp] = bank([P, 2, 2, P], "pair")
             for g in (2 * gp, 2 * gp + 1):
-                turn(xb[x][:].bitcast(F32), g, pairs[x, gp])
+                turn(xb[x][:].bitcast(F32), g, pairs[x, gp], False)
 
         def scale_x(x, g):
             if g == 0:
@@ -138,7 +139,10 @@ def tile_matchingnet_pa_w4_kernel(tc, h3_bytes, h3_scale, W4_words, W4_scales, b
 
         def bias4(x, c):
             ys[x, c] = work.tile([P, 512], F32, name="y", bufs=3)
-            nc.vector.tensor_tensor(out=ys[x, c][:], in0=accs[x, c][:], in1=b4_t[:, 512 * c:512 * (c + 1)], op=ALU.add)
+            pairs_apart = "p (m u e) -> p u m e"
+            nc.vector.tensor_tensor(
+                out=ys[x, c][:].rearrange("p (u m e) -> p u m e", u=2, e=2), in0=accs[x, c][:].rearrange(pairs_apart, u=2, e=2),
+                in1=b4_t[:, 512 * c:512 * (c + 1)].rearrange(pairs_apart, u=2, e=2), op=ALU.add)
 
         def leak4(x, c):
             if c == 0:
@@ -149,7 +153,7 @@ def tile_matchingnet_pa_w4_kernel(tc, h3_bytes, h3_scale, W4_words, W4_scales, b
         def turn_h(x, gp):
             pair = bank([P, 2, 2, P], "pair4")
             for g in (2 * gp, 2 * gp + 1):
-                turn(h4[x][:].bitcast(F32), g, pair)
+                turn(h4[x][:].bitcast(F32), g, pair, True)
             if gp == 0:
                 grouped4[x] = work.tile([P, GROUPS, P, 4], BF16, name="grouped4", align_bytes=64)
             nc.scalar.copy(
@@ -183,7 +187,20 @@ def tile_matchingnet_pa_w4_kernel(tc, h3_bytes, h3_scale, W4_words, W4_scales, b
                 nc.vector.scalar_tensor_tensor(out=A[x][:, 512 * c:512 * (c + 1)], in0=zs[x, c][:], scalar=FLOOR, in1=ns[x, c][:], op0=ALU.max, op1=ALU.add)
             nc.scalar.copy(AT[x][:].rearrange("p (a c i) -> p a i c", a=8, c=4), A[x][:].rearrange("p (i a c) -> p a i c", a=8, c=4))
 
-        slots = 2 * ITERS * TILES
+        halves = 2 * ITERS
+        lead = 0
+        seq = []
+        for b in range(halves + lead):
+            for x in range(TILES):
+                h = b if x < 2 else b - lead
+                seq.append(h * TILES + x if 0 <= h < halves else None)
+        at = [0]
+
+        def advance(count):
+            for p in range(at[0], at[0] + count):
+                slot(p)
+            at[0] += count
+
         prod, turned, sums, inv, turned_sb, rows_t = {}, {}, {}, {}, {}, {}
 
         def source(n):
@@ -241,8 +258,13 @@ def tile_matchingnet_pa_w4_kernel(tc, h3_bytes, h3_scale, W4_words, W4_scales, b
                 nc.scalar.activation(o[:, cols], r[:, cols], ACTF.Copy, scale=u[:, a:a + 1])
             nc.sync.dma_start(out=out2[x * P:(x + 1) * P, :], in_=o[:])
 
-        def slot(n):
-            live, full = n < slots, TILES <= n < slots
+        def key(p):
+            return seq[p] if 0 <= p < len(seq) else None
+
+        def slot(p):
+            n, n1, n2, n3 = key(p), key(p - 1), key(p - 2), key(p - 3)
+            live = n is not None
+            full = live and n >= TILES
             if live:
                 turned[n] = bank([P, P], "turned")
                 prod[n] = work.tile([P, DOUT], F32, name="prod", bufs=4) if full else A[n]
@@ -250,8 +272,8 @@ def tile_matchingnet_pa_w4_kernel(tc, h3_bytes, h3_scale, W4_words, W4_scales, b
                 scale_vec(n, 0, 12)
             if full:
                 scale_act(n, 20, 24)
-            if 0 <= n - 3 < slots:
-                clamp(n - 3)
+            if n3 is not None:
+                clamp(n3)
             if full:
                 scale_act(n, 24, 28)
             if live:
@@ -270,22 +292,22 @@ def tile_matchingnet_pa_w4_kernel(tc, h3_bytes, h3_scale, W4_words, W4_scales, b
                 turn_chunk(n, 3, False, False)
             if full:
                 scale_act(n, 28, 32)
-            if 0 <= n - 2 < slots:
-                invert(n - 2)
+            if n2 is not None:
+                invert(n2)
             if full:
                 scale_act(n, 17, 20)
             if live:
                 turn_chunk(n, 4, False, False)
             if live:
                 turn_chunk(n, 7, False, True)
-            if 0 <= n - 1 < slots:
-                take(n - 1)
-            if 0 <= n - 1 < slots:
-                fold_sum(n - 1)
-            if live and n >= slots - TILES:
+            if n1 is not None:
+                take(n1)
+            if n1 is not None:
+                fold_sum(n1)
+            if live and n >= (halves - 1) * TILES:
                 row_scaled(n % TILES)
-            if n - 3 >= slots - TILES:
-                finish((n - 3) % TILES)
+            if n3 is not None and n3 >= (halves - 1) * TILES:
+                finish(n3 % TILES)
 
         for i in range(FOLD // N):
             nc.vector.tensor_reduce(out=fold[:, N * i:N * (i + 1)], in_=ident[:].rearrange("p (q j) -> p j q", q=4), axis=AX.X, op=ALU.add)
@@ -304,8 +326,8 @@ def tile_matchingnet_pa_w4_kernel(tc, h3_bytes, h3_scale, W4_words, W4_scales, b
         for g in range(GROUPS):
             scale_x(1, g)
         quant_x(1)
-        for x in range(TILES):
-            ahead = x + 1 if 0 < x < TILES - 1 else 0
+        for x in range(TILES - 1):
+            ahead = x + 1 if x > 0 else 0
             layer4(x, 0)
             bias4(x, 0)
             layer4(x, 1)
@@ -322,10 +344,6 @@ def tile_matchingnet_pa_w4_kernel(tc, h3_bytes, h3_scale, W4_words, W4_scales, b
             if x > 0:
                 quant_h(x - 1)
             leak4(x, 1)
-            if x == 3:
-                log5(0)
-                log5(1)
-                soft5(0)
             layer4(x, 2)
             if x > 0:
                 layer5(x - 1, 0)
@@ -333,8 +351,6 @@ def tile_matchingnet_pa_w4_kernel(tc, h3_bytes, h3_scale, W4_words, W4_scales, b
             if ahead:
                 scale_x(ahead, 2)
             leak4(x, 2)
-            if x == 3:
-                soft5(1)
             if x > 0:
                 bias5(x - 1, 0)
             layer4(x, 3)
@@ -349,22 +365,41 @@ def tile_matchingnet_pa_w4_kernel(tc, h3_bytes, h3_scale, W4_words, W4_scales, b
             leak4(x, 3)
             if x > 0:
                 bias5(x - 1, 1)
-            if 0 <= x < 2:
+            if x < 2:
                 for g in range(GROUPS):
                     widen(x + 2, g)
-        turn_h(3, 1)
+        layer4(3, 0)
+        turn_h(2, 1)
+        bias4(3, 0)
+        layer4(3, 1)
+        log5(0)
+        log5(1)
+        quant_h(2)
+        leak4(3, 0)
+        bias4(3, 1)
+        layer4(3, 2)
+        soft5(0)
+        leak4(3, 1)
+        layer5(2, 0)
+        bias4(3, 2)
+        layer4(3, 3)
+        turn_h(3, 0)
+        bias5(2, 0)
+        leak4(3, 2)
+        layer5(2, 1)
+        bias4(3, 3)
         quant_h(3, 0, 2)
+        leak4(3, 3)
+        turn_h(3, 1)
+        soft5(1)
+        bias5(2, 1)
         quant_h(3, 2, 4)
         layer5(3, 0)
         layer5(3, 1)
         bias5(3, 0)
         bias5(3, 1)
-        slot(0)
-        slot(1)
         log5(2)
-        soft5(2)
-        slot(2)
         log5(3)
+        soft5(2)
         soft5(3)
-        for n in range(3, slots + 4):
-            slot(n)
+        advance(len(seq) + 4)

@@ -18,7 +18,7 @@ AX = mybir.AxisListType
 P = 128
 B, HID, DOUT, N, ITERS = 512, 2048, 1024, 32, 10
 SLOPE, EPS, FLOOR = 0.01, 1e-8, 1e-30
-FOLD = 160
+NARROW, WIDE = 64, 256
 GROUPS = HID // 512
 TILES = B // P
 FLOPS = 2 * B * HID * HID + 2 * B * HID * DOUT
@@ -37,10 +37,11 @@ def tile_matchingnet_pa_w4_kernel(tc, h3_bytes, h3_scale, W4_words, W4_scales, b
 
         ident = keep.tile([P, P], F32, name="ident")
         make_identity(nc, ident[:])
-        fold = keep.tile([P, FOLD], F32, name="fold")
+        fold = keep.tile([P, WIDE], F32, name="fold")
+        fold_rows = keep.tile([P, WIDE], F32, name="fold_rows")
 
-        w4s = keep.tile([P, GROUPS, HID], U8, name="w4s", align_bytes=64)
-        w5s = keep.tile([P, GROUPS, DOUT], U8, name="w5s", align_bytes=64)
+        w4s = [keep.tile([P, GROUPS, 1024], U8, name="w4s_%d" % c, align_bytes=64) for c in range(2)]
+        w5s = [keep.tile([P, GROUPS, 1024], U8, name="w5s_%d" % c, align_bytes=64) for c in range(1)]
         w4 = [keep.tile([P, GROUPS, 1024], U8, name="w4_%d" % c, align_bytes=64) for c in range(4)]
         w5 = [keep.tile([P, GROUPS, 1024], U8, name="w5_%d" % c, align_bytes=64) for c in range(2)]
         b4_t = keep.tile([P, HID], BF16, name="b4_t")
@@ -48,24 +49,24 @@ def tile_matchingnet_pa_w4_kernel(tc, h3_bytes, h3_scale, W4_words, W4_scales, b
         sc = keep.tile([P, GROUPS, 4], F32, name="sc")
         x_bytes = [keep.tile([P, HID], U8, name="x_bytes%d" % x, align_bytes=64) for x in range(TILES)]
 
-        nc.gpsimd.memset(w5s[:].rearrange("p g n -> p (g n)").bitcast(I32), 0)
+        nc.gpsimd.memset(w5s[0][:].rearrange("p g n -> p (g n)").bitcast(I32), 0)
 
         def load_x(x):
             nc.sync.dma_start(out=x_bytes[x][:], in_=h3_bytes[x * P:(x + 1) * P, :])
 
-        def load_scales(dst, src):
-            for q in range(4):
-                nc.sync.dma_start(out=dst[32 * q:32 * q + 4, :, :].bitcast(I32), in_=src[:, 4 * q:4 * q + 4, :].rearrange("g q n -> q g n").bitcast(I32))
 
         ctx.enter_context(tc.manual_schedule())
         warm = keep.tile([P, 1], F32, name="warm")
         nc.vector.memset(warm[:], 1.0)
         nc.scalar.activation(warm[:], warm[:], ACTF.Exp)
-        nc.vector.memset(w4s[:].rearrange("p g n -> p (g n)").bitcast(I32), 0)
+        nc.vector.memset(w4s[0][:].rearrange("p g n -> p (g n)").bitcast(I32), 0)
+        nc.vector.memset(w4s[1][:].rearrange("p g n -> p (g n)").bitcast(I32), 0)
         load_x(0)
         nc.sync.dma_start(out=sc[:], in_=h3_scale.rearrange("o (g p t) -> p (o g) t", p=P, t=4))
-        load_x(1)
-        load_scales(w4s, W4_scales)
+
+        def load_scales(dst, src, c0, c1):
+            for q in range(4):
+                nc.sync.dma_start(out=dst[32 * q:32 * q + 4, :, :].bitcast(I32), in_=src[:, 4 * q:4 * q + 4, c0:c1].rearrange("g q n -> q g n").bitcast(I32))
 
         def load_words(dst, src, c):
             nc.sync.dma_start(out=dst[c][:], in_=src[:, :, 1024 * c:1024 * (c + 1)].rearrange("g p n -> p g n"))
@@ -73,14 +74,17 @@ def tile_matchingnet_pa_w4_kernel(tc, h3_bytes, h3_scale, W4_words, W4_scales, b
         def load_bias(dst, src, c0, c1):
             nc.sync.dma_start(out=dst[:, c0:c1], in_=src[c0:c1].partition_broadcast(P))
 
-        load_words(w4, W4_words, 0)
+        load_x(1)
+        load_scales(w4s[0], W4_scales, 0, 1024)
         load_bias(b4_t, b4, 0, 1024)
+        load_words(w4, W4_words, 0)
         load_words(w4, W4_words, 1)
+        load_scales(w4s[1], W4_scales, 1024, HID)
         load_words(w4, W4_words, 2)
         load_bias(b4_t, b4, 1024, 2048)
         load_words(w4, W4_words, 3)
         load_x(2)
-        load_scales(w5s, W5_scales)
+        load_scales(w5s[0], W5_scales, 0, DOUT)
         load_words(w5, W5_words, 0)
         load_words(w5, W5_words, 1)
         load_x(3)
@@ -130,7 +134,7 @@ def tile_matchingnet_pa_w4_kernel(tc, h3_bytes, h3_scale, W4_words, W4_scales, b
             for g in range(GROUPS):
                 nc.tensor.matmul_mx(
                     out=acc[:], lhsT=cw[:, P * g:P * (g + 1)].bitcast(FP8X4), lhsT_scale=sw[:, P * g:P * (g + 1)],
-                    rhs=w[c][:, g, :].bitcast(FP4X4), rhs_scale=ws[:, g, 512 * c:512 * (c + 1)],
+                    rhs=w[c][:, g, :].bitcast(FP4X4), rhs_scale=ws[c // 2][:, g, 512 * (c % 2):512 * (c % 2 + 1)],
                     start=(g == 0), stop=(g == GROUPS - 1))
 
         def layer4(x, c):
@@ -171,21 +175,37 @@ def tile_matchingnet_pa_w4_kernel(tc, h3_bytes, h3_scale, W4_words, W4_scales, b
             accs[x, c] = bank([P, 512], "acc2")
             layer(accs[x, c], c, codes4[x], scales4[x], w5, w5s)
 
-        def bias5(x, c):
-            zs[x, c] = work.tile([P, 512], F32, name="z", bufs=8)
-            ns[x, c] = work.tile([P, 512], F32, name="n", bufs=8)
-            nc.vector.tensor_tensor(out=zs[x, c][:], in0=accs[x, c][:], in1=b5_t[:, 512 * c:512 * (c + 1)], op=ALU.add)
-            nc.scalar.activation(ns[x, c][:], zs[x, c][:], ACTF.Abs)
-            nc.scalar.activation(ns[x, c][:], ns[x, c][:], ACTF.Exp, scale=-1.0)
+        def bias5(x, c0, c1):
+            if c0 == 0:
+                zs[x] = work.tile([P, DOUT], F32, name="z", bufs=4)
+                ns[x] = work.tile([P, DOUT], F32, name="n", bufs=4)
+            nc.vector.tensor_tensor(out=zs[x][:, c0:c1], in0=accs[x, c0 // 512][:, c0 % 512:c0 % 512 + c1 - c0], in1=b5_t[:, c0:c1], op=ALU.add)
 
-        def log5(x):
-            for c in range(2):
-                nc.scalar.activation(ns[x, c][:], ns[x, c][:], ACTF.Ln, bias=1.0)
+        def exp5(x, c0, c1, on_vector):
+            z, n = zs[x][:, c0:c1], ns[x][:, c0:c1]
+            if on_vector:
+                nc.vector.scalar_tensor_tensor(out=n, in0=z, scalar=-1.0, in1=z, op0=ALU.mult, op1=ALU.min)
+                nc.scalar.activation(n, n, ACTF.Exp)
+            else:
+                nc.scalar.activation(n, z, ACTF.Abs)
+                nc.scalar.activation(n, n, ACTF.Exp, scale=-1.0)
 
-        def soft5(x):
-            for c in range(2):
-                nc.vector.scalar_tensor_tensor(out=A[x][:, 512 * c:512 * (c + 1)], in0=zs[x, c][:], scalar=FLOOR, in1=ns[x, c][:], op0=ALU.max, op1=ALU.add)
-            nc.scalar.copy(AT[x][:].rearrange("p (a c i) -> p a i c", a=8, c=4), A[x][:].rearrange("p (i a c) -> p a i c", a=8, c=4))
+        def log5(x, step=512):
+            for c in range(0, DOUT, step):
+                nc.scalar.activation(ns[x][:, c:c + step], ns[x][:, c:c + step], ACTF.Ln, bias=1.0)
+
+        def soft5(x, step=512):
+            for c in range(0, DOUT, step):
+                cols = slice(c, c + step)
+                nc.vector.scalar_tensor_tensor(out=A[x][:, cols], in0=zs[x][:, cols], scalar=FLOOR, in1=ns[x][:, cols], op0=ALU.max, op1=ALU.add)
+
+        def flip5(x, on_vector):
+            dst = AT[x][:].rearrange("p (a c i) -> p a i c", a=8, c=4)
+            src = A[x][:].rearrange("p (i a c) -> p a i c", a=8, c=4)
+            if on_vector:
+                nc.vector.tensor_copy(out=dst, in_=src)
+            else:
+                nc.scalar.copy(dst, src)
 
         halves = 2 * ITERS
         lead = 0
@@ -226,91 +246,129 @@ def tile_matchingnet_pa_w4_kernel(tc, h3_bytes, h3_scale, W4_words, W4_scales, b
             nc.scalar.copy(turned_sb[n][:], turned[n][:])
 
         def fold_sum(n):
-            sums[n] = bank([P, FOLD], "sums")
-            nc.tensor.matmul(out=sums[n][:], lhsT=turned_sb[n][:], rhs=fold[:], start=True, stop=True)
+            width = WIDE if n < TILES else 128 if n < 2 * TILES else NARROW
+            sums[n] = bank([P, width], "sums")
+            nc.tensor.matmul(out=sums[n][:], lhsT=turned_sb[n][:], rhs=(fold_rows if n >= last else fold)[:, 0:width], start=True, stop=True)
 
-        raw = {}
+        floor_of, half_inv = {}, {}
+        exact = (halves - 2) * TILES
 
-        def invert(n):
-            raw[n] = work.tile([P, N], F32, name="raw", bufs=16)
-            nc.vector.reciprocal(raw[n][:], sums[n][:, 0:N])
+        def root_table():
+            nc.scalar.activation(warm[:], warm[:], ACTF.Abs_reciprocal_sqrt)
 
         def clamp(n):
-            inv[n] = work.tile([P, N], F32, name="inv", bufs=16)
+            floor_of[n] = work.tile([P, N], F32, name="floor", bufs=16)
             if n < 2 * TILES:
-                nc.vector.tensor_scalar(out=inv[n][:], in0=raw[n][:], scalar1=1.0 / EPS, scalar2=None, op0=ALU.min)
+                nc.vector.tensor_scalar(out=floor_of[n][:], in0=sums[n][:, 0:N], scalar1=EPS, scalar2=None, op0=ALU.max)
             else:
-                nc.vector.scalar_tensor_tensor(out=inv[n][:], in0=inv[n - 2 * TILES][:], scalar=1.0 / EPS, in1=raw[n][:], op0=ALU.mult, op1=ALU.min)
+                nc.vector.scalar_tensor_tensor(out=floor_of[n][:], in0=floor_of[n - 2 * TILES][:], scalar=EPS, in1=sums[n][:, 0:N], op0=ALU.mult, op1=ALU.max)
 
-        def row_scaled(x):
-            v = inv[(2 * ITERS - 2) * TILES + x]
-            rows_t[x] = work.tile([P, DOUT], F32, name="r", bufs=4)
-            nc.vector.tensor_tensor(out=rows_t[x][:].rearrange("p (i j) -> p i j", j=N), in0=A[x][:].rearrange("p (i j) -> p i j", j=N), in1=v[:].unsqueeze(1).to_broadcast([P, N, N]), op=ALU.mult)
+        def root(n):
+            inv[n] = work.tile([P, N], F32, name="inv", bufs=16)
+            if n >= exact:
+                nc.vector.reciprocal(inv[n][:], floor_of[n][:])
+                return
+            half_inv[n] = work.tile([P, N], F32, name="half_inv", bufs=4)
+            nc.scalar.activation(half_inv[n][:], floor_of[n][:], ACTF.Abs_reciprocal_sqrt)
 
-        def finish(x):
-            u = inv[(2 * ITERS - 1) * TILES + x]
-            r = rows_t[x]
-            o = work.tile([P, DOUT], F32, name="o", bufs=2)
+        def square(n):
+            if n < exact:
+                nc.scalar.activation(inv[n][:], half_inv[n][:], ACTF.Square)
+
+        last = (halves - 1) * TILES
+
+        def row_scaled(n):
+            rows_t[n] = work.tile([P, DOUT], F32, name="r", bufs=4)
+            nc.vector.tensor_tensor(
+                out=rows_t[n][:].rearrange("p (i j) -> p i j", j=N), in0=A[n % TILES][:].rearrange("p (i j) -> p i j", j=N),
+                in1=inv[n - TILES][:].unsqueeze(1).to_broadcast([P, N, N]), op=ALU.mult)
+
+        def turn_row(n, k):
+            nc.tensor.matmul(out=turned[n][:], lhsT=rows_t[n][:, k:DOUT:8], rhs=ident[:], is_transpose=True, start=(k == 0), stop=(k == 7))
+
+        def finish(n):
+            r, u = rows_t[n], inv[n]
+            o = work.tile([P, DOUT], F32, name="o", bufs=4)
             cut = 18
+            where = out2[n % TILES * P:(n % TILES + 1) * P, :]
             nc.vector.tensor_tensor(out=o[:, 0:N * cut].rearrange("p (i j) -> p i j", j=N), in0=r[:, 0:N * cut].rearrange("p (i j) -> p i j", j=N), in1=u[:, 0:cut].unsqueeze(2).to_broadcast([P, cut, N]), op=ALU.mult)
+            nc.sync.dma_start(out=where[:, 0:N * cut], in_=o[:, 0:N * cut])
             for a in range(cut, N):
                 cols = slice(N * a, N * (a + 1))
                 nc.scalar.activation(o[:, cols], r[:, cols], ACTF.Copy, scale=u[:, a:a + 1])
-            nc.sync.dma_start(out=out2[x * P:(x + 1) * P, :], in_=o[:])
+            nc.sync.dma_start(out=where[:, N * cut:], in_=o[:, N * cut:])
 
         def key(p):
             return seq[p] if 0 <= p < len(seq) else None
 
-        def slot(p):
+        def last_slot(p):
             n, n1, n2, n3 = key(p), key(p - 1), key(p - 2), key(p - 3)
+            if n is not None:
+                turned[n] = bank([P, P], "turned")
+                row_scaled(n)
+                for k in range(8):
+                    turn_row(n, k)
+            if n1 is not None:
+                take(n1)
+                fold_sum(n1)
+            if n3 is not None:
+                root(n3)
+                square(n3)
+                if n3 >= last:
+                    finish(n3)
+            if n2 is not None:
+                clamp(n2)
+
+        def slot(p):
+            if p >= last:
+                last_slot(p)
+                return
+            n, n1, n2, n3, n4 = key(p), key(p - 1), key(p - 2), key(p - 3), key(p - 4)
             live = n is not None
             full = live and n >= TILES
             if live:
                 turned[n] = bank([P, P], "turned")
                 prod[n] = work.tile([P, DOUT], F32, name="prod", bufs=4) if full else A[n]
             if full:
+                scale_act(n, 28, 32)
+            if live:
+                turn_chunk(n, 7, True, False)
+            if full:
                 scale_vec(n, 0, 12)
-            if full:
-                scale_act(n, 20, 24)
-            if n3 is not None:
-                clamp(n3)
-            if full:
-                scale_act(n, 24, 28)
-            if live:
-                turn_chunk(n, 6, True, False)
-            if live:
-                turn_chunk(n, 5, False, False)
             if live:
                 turn_chunk(n, 1, False, False)
             if live:
+                turn_chunk(n, 2, False, False)
+            if n3 is not None:
+                root(n3)
+            if full:
+                scale_vec(n, 12, 21)
+            if full:
+                scale_act(n, 24, 28)
+            if live:
+                turn_chunk(n, 6, False, False)
+            if live:
                 turn_chunk(n, 0, False, False)
             if live:
-                turn_chunk(n, 2, False, False)
-            if full:
-                scale_vec(n, 12, 17)
-            if live:
-                turn_chunk(n, 3, False, False)
-            if full:
-                scale_act(n, 28, 32)
-            if n2 is not None:
-                invert(n2)
-            if full:
-                scale_act(n, 17, 20)
-            if live:
                 turn_chunk(n, 4, False, False)
+            if n2 is not None:
+                clamp(n2)
+            if n3 is not None:
+                square(n3)
+            if full:
+                scale_act(n, 21, 24)
             if live:
-                turn_chunk(n, 7, False, True)
+                turn_chunk(n, 5, False, False)
+            if live:
+                turn_chunk(n, 3, False, True)
             if n1 is not None:
                 take(n1)
             if n1 is not None:
                 fold_sum(n1)
-            if live and n >= (halves - 1) * TILES:
-                row_scaled(n % TILES)
-            if n3 is not None and n3 >= (halves - 1) * TILES:
-                finish(n3 % TILES)
 
-        for i in range(FOLD // N):
+        for i in range(WIDE // N):
             nc.vector.tensor_reduce(out=fold[:, N * i:N * (i + 1)], in_=ident[:].rearrange("p (q j) -> p j q", q=4), axis=AX.X, op=ALU.add)
+            nc.vector.tensor_reduce(out=fold_rows[:, N * i:N * (i + 1)], in_=ident[:].rearrange("p (i q) -> p i q", q=4), axis=AX.X, op=ALU.add)
         for g in range(GROUPS):
             widen(0, g, g % 2 == 1)
         turn_x(0, 0)
@@ -319,87 +377,110 @@ def tile_matchingnet_pa_w4_kernel(tc, h3_bytes, h3_scale, W4_words, W4_scales, b
             widen(1, g)
         for g in range(GROUPS):
             scale_x(0, g)
-        quant_x(0, 0, 2)
         turn_x(1, 0)
-        quant_x(0, 2, 4)
         turn_x(1, 1)
-        for g in range(GROUPS):
-            scale_x(1, g)
+        quant_x(0, 0, 2)
+        quant_x(0, 2, 4)
+        scale_x(1, 0)
+        scale_x(1, 1)
+        layer4(0, 0)
+        scale_x(1, 2)
+        layer4(0, 1)
+        bias4(0, 0)
+        scale_x(1, 3)
+        layer4(0, 2)
+        leak4(0, 0)
+        bias4(0, 1)
         quant_x(1)
-        for x in range(TILES - 1):
-            ahead = x + 1 if x > 0 else 0
-            layer4(x, 0)
+        leak4(0, 1)
+        layer4(0, 3)
+        bias4(0, 2)
+        for g in range(GROUPS):
+            widen(2, g)
+        turn_h(0, 0)
+        turn_x(2, 0)
+        turn_x(2, 1)
+        bias4(0, 3)
+        leak4(0, 2)
+        leak4(0, 3)
+        layer4(1, 0)
+        turn_h(0, 1)
+        layer4(1, 1)
+        for g in range(GROUPS):
+            widen(3, g)
+        for x in (1, 2):
+            scale_x(x + 1, 0)
+            scale_x(x + 1, 1)
+            scale_x(x + 1, 2)
             bias4(x, 0)
-            layer4(x, 1)
-            if x > 0:
-                turn_h(x - 1, 1)
-            if ahead:
-                turn_x(ahead, 0)
-                turn_x(ahead, 1)
-                scale_x(ahead, 0)
+            quant_h(x - 1)
+            scale_x(x + 1, 3)
+            layer5(x - 1, 0)
             leak4(x, 0)
             bias4(x, 1)
-            if ahead:
-                scale_x(ahead, 1)
-            if x > 0:
-                quant_h(x - 1)
-            leak4(x, 1)
             layer4(x, 2)
-            if x > 0:
-                layer5(x - 1, 0)
-            bias4(x, 2)
-            if ahead:
-                scale_x(ahead, 2)
-            leak4(x, 2)
-            if x > 0:
-                bias5(x - 1, 0)
+            quant_x(x + 1)
+            leak4(x, 1)
+            bias5(x - 1, 0, 512)
+            exp5(x - 1, 0, 512, False)
             layer4(x, 3)
-            if x > 0:
-                layer5(x - 1, 1)
+            bias4(x, 2)
+            layer5(x - 1, 1)
             turn_h(x, 0)
-            if ahead:
-                scale_x(ahead, 3)
             bias4(x, 3)
-            if ahead:
-                quant_x(ahead)
+            leak4(x, 2)
+            bias5(x - 1, 512, DOUT)
+            exp5(x - 1, 512, DOUT, False)
             leak4(x, 3)
-            if x > 0:
-                bias5(x - 1, 1)
-            if x < 2:
-                for g in range(GROUPS):
-                    widen(x + 2, g)
-        layer4(3, 0)
-        turn_h(2, 1)
+            if x == 1:
+                turn_x(3, 0)
+                turn_x(3, 1)
+            layer4(x + 1, 0)
+            turn_h(x, 1)
+            layer4(x + 1, 1)
         bias4(3, 0)
-        layer4(3, 1)
-        log5(0)
-        log5(1)
-        quant_h(2)
         leak4(3, 0)
-        bias4(3, 1)
+        quant_h(2)
         layer4(3, 2)
-        soft5(0)
-        leak4(3, 1)
-        layer5(2, 0)
-        bias4(3, 2)
+        bias4(3, 1)
         layer4(3, 3)
-        turn_h(3, 0)
-        bias5(2, 0)
-        leak4(3, 2)
-        layer5(2, 1)
+        bias4(3, 2)
+        layer5(2, 0)
+        log5(0)
+        leak4(3, 1)
         bias4(3, 3)
-        quant_h(3, 0, 2)
+        turn_h(3, 0)
+        layer5(2, 1)
+        leak4(3, 2)
+        log5(1)
         leak4(3, 3)
+        bias5(2, 0, 512)
+        soft5(0)
+        bias5(2, 512, DOUT)
         turn_h(3, 1)
-        soft5(1)
-        bias5(2, 1)
+        quant_h(3, 0, 2)
         quant_h(3, 2, 4)
+        exp5(2, 512, DOUT, True)
         layer5(3, 0)
+        soft5(1)
+        bias5(3, 0, 256)
+        exp5(2, 0, 512, True)
+        bias5(3, 256, 512)
+        exp5(3, 0, 256, True)
         layer5(3, 1)
-        bias5(3, 0)
-        bias5(3, 1)
+        bias5(3, 512, 768)
+        advance(2)
+        exp5(3, 256, 512, True)
+        bias5(3, 768, DOUT)
+        exp5(3, 512, 768, True)
+        exp5(3, 768, DOUT, True)
+        flip5(0, True)
+        flip5(1, True)
         log5(2)
-        log5(3)
         soft5(2)
-        soft5(3)
-        advance(len(seq) + 4)
+        log5(3, 256)
+        root_table()
+        soft5(3, 256)
+        flip5(2, True)
+        flip5(3, True)
+        advance(len(seq) + 4 - at[0])

from contextlib import ExitStack

import concourse.mybir as mybir
from concourse.masks import make_identity

F32 = mybir.dt.float32
BF16 = mybir.dt.bfloat16
I32 = mybir.dt.int32
U32 = mybir.dt.uint32
U8 = mybir.dt.uint8
E4M3 = mybir.dt.float8_e4m3fn
FP8X4 = mybir.dt.float8_e4m3fn_x4
FP4X4 = mybir.dt.float4_e2m1fn_x4
ALU = mybir.AluOpType
ACTF = mybir.ActivationFunctionType
AX = mybir.AxisListType

P = 128
B, HID, DOUT, N, ITERS = 512, 2048, 1024, 32, 10
SLOPE, EPS, FLOOR = 0.01, 1e-8, 1e-30
NARROW, WIDE = 64, 256
GROUPS = HID // 512
TILES = B // P
FLOPS = 2 * B * HID * HID + 2 * B * HID * DOUT


def tile_matchingnet_pa_w4_kernel(tc, h3_bytes, h3_scale, W4_words, W4_scales, b4, W5_words, W5_scales, b5, out):
    nc = tc.nc
    out2 = out.rearrange("b i j -> b (i j)")
    with ExitStack() as ctx:
        keep = ctx.enter_context(tc.tile_pool(name="keep", bufs=1))
        work = ctx.enter_context(tc.tile_pool(name="work", bufs=2))
        psum = ctx.enter_context(tc.psum_pool(name="psum", bufs=8))

        def bank(shape, name):
            return psum.tile(shape, F32, tag="bank", name=name)

        ident = keep.tile([P, P], F32, name="ident")
        make_identity(nc, ident[:])
        fold = keep.tile([P, WIDE], F32, name="fold")
        fold_rows = keep.tile([P, WIDE], F32, name="fold_rows")

        w4s = [keep.tile([P, GROUPS, 1024], U8, name="w4s_%d" % c, align_bytes=64) for c in range(2)]
        w5s = [keep.tile([P, GROUPS, 1024], U8, name="w5s_%d" % c, align_bytes=64) for c in range(1)]
        w4 = [keep.tile([P, GROUPS, 1024], U8, name="w4_%d" % c, align_bytes=64) for c in range(4)]
        w5 = [keep.tile([P, GROUPS, 1024], U8, name="w5_%d" % c, align_bytes=64) for c in range(2)]
        b4_t = keep.tile([P, HID], BF16, name="b4_t")
        b5_t = keep.tile([P, DOUT], BF16, name="b5_t")
        sc = keep.tile([P, GROUPS, 4], F32, name="sc")
        x_bytes = [keep.tile([P, HID], U8, name="x_bytes%d" % x, align_bytes=64) for x in range(TILES)]

        nc.gpsimd.memset(w5s[0][:].rearrange("p g n -> p (g n)").bitcast(I32), 0)

        def load_x(x):
            nc.sync.dma_start(out=x_bytes[x][:], in_=h3_bytes[x * P:(x + 1) * P, :])


        ctx.enter_context(tc.manual_schedule())
        warm = keep.tile([P, 1], F32, name="warm")
        nc.vector.memset(warm[:], 1.0)
        nc.scalar.activation(warm[:], warm[:], ACTF.Exp)
        nc.vector.memset(w4s[0][:].rearrange("p g n -> p (g n)").bitcast(I32), 0)
        nc.vector.memset(w4s[1][:].rearrange("p g n -> p (g n)").bitcast(I32), 0)
        load_x(0)
        nc.sync.dma_start(out=sc[:], in_=h3_scale.rearrange("o (g p t) -> p (o g) t", p=P, t=4))

        def load_scales(dst, src, c0, c1):
            for q in range(4):
                nc.sync.dma_start(out=dst[32 * q:32 * q + 4, :, :].bitcast(I32), in_=src[:, 4 * q:4 * q + 4, c0:c1].rearrange("g q n -> q g n").bitcast(I32))

        def load_words(dst, src, c):
            nc.sync.dma_start(out=dst[c][:], in_=src[:, :, 1024 * c:1024 * (c + 1)].rearrange("g p n -> p g n"))

        def load_bias(dst, src, c0, c1):
            nc.sync.dma_start(out=dst[:, c0:c1], in_=src[c0:c1].partition_broadcast(P))

        load_x(1)
        load_scales(w4s[0], W4_scales, 0, 1024)
        load_bias(b4_t, b4, 0, 1024)
        load_words(w4, W4_words, 0)
        load_words(w4, W4_words, 1)
        load_scales(w4s[1], W4_scales, 1024, HID)
        load_words(w4, W4_words, 2)
        load_bias(b4_t, b4, 1024, 2048)
        load_words(w4, W4_words, 3)
        load_x(2)
        load_scales(w5s[0], W5_scales, 0, DOUT)
        load_words(w5, W5_words, 0)
        load_words(w5, W5_words, 1)
        load_x(3)
        load_bias(b5_t, b5, 0, DOUT)

        A = [keep.tile([P, DOUT], F32, name="A%d" % x) for x in range(TILES)]
        AT = [keep.tile([P, DOUT], F32, name="AT%d" % x) for x in range(TILES)]

        xb, grouped, codes, scales, pairs, h4, grouped4, codes4, scales4, accs, ys, zs, ns = {}, {}, {}, {}, {}, {}, {}, {}, {}, {}, {}, {}, {}

        def turn(words, g, pair, apart):
            for u in range(2):
                cols = slice(256 * g + 128 * u, 256 * g + 128 * (u + 1)) if apart else slice(256 * g + u, 256 * (g + 1), 2)
                nc.tensor.transpose(pair[:, g % 2, u, :], words[:, cols], ident[:])

        def widen(x, g, on_vector=False):
            if g == 0:
                xb[x] = work.tile([P, HID], BF16, name="xb", align_bytes=64)
            dst, src = xb[x][:, 512 * g:512 * (g + 1)], x_bytes[x][:, 512 * g:512 * (g + 1)].bitcast(E4M3)
            if on_vector:
                nc.vector.tensor_copy(out=dst, in_=src)
            else:
                nc.scalar.copy(dst, src)

        def turn_x(x, gp):
            pairs[x, gp] = bank([P, 2, 2, P], "pair")
            for g in (2 * gp, 2 * gp + 1):
                turn(xb[x][:].bitcast(F32), g, pairs[x, gp], False)

        def scale_x(x, g):
            if g == 0:
                grouped[x] = work.tile([P, GROUPS, P, 4], BF16, name="grouped", align_bytes=64)
            nc.vector.tensor_tensor(
                out=grouped[x][:, g, :, :].rearrange("p r (u e) -> p r u e", e=2),
                in0=pairs[x, g // 2][:, g % 2, :, :].rearrange("p u r -> p (u r)").bitcast(BF16).rearrange("p (u r e) -> p r u e", u=2, e=2),
                in1=sc[:, g, :].rearrange("p (u e) -> p u e", e=2).unsqueeze(1).to_broadcast([P, P, 2, 2]),
                op=ALU.mult)

        def quant_x(x, g0=0, g1=GROUPS):
            if g0 == 0:
                codes[x] = work.tile([P, GROUPS * P], U32, name="codes", align_bytes=64)
                scales[x] = work.tile([P, GROUPS * P], U8, name="scales", align_bytes=64)
            cols = slice(P * g0, P * g1)
            nc.vector.quantize_mx(out=codes[x][:, cols].bitcast(FP8X4), scales=scales[x][:, cols], in_=grouped[x][:, g0:g1, :, :].rearrange("p g r t -> p (g r t)"))

        def layer(acc, c, cw, sw, w, ws):
            for g in range(GROUPS):
                nc.tensor.matmul_mx(
                    out=acc[:], lhsT=cw[:, P * g:P * (g + 1)].bitcast(FP8X4), lhsT_scale=sw[:, P * g:P * (g + 1)],
                    rhs=w[c][:, g, :].bitcast(FP4X4), rhs_scale=ws[c // 2][:, g, 512 * (c % 2):512 * (c % 2 + 1)],
                    start=(g == 0), stop=(g == GROUPS - 1))

        def layer4(x, c):
            accs[x, c] = bank([P, 512], "acc")
            layer(accs[x, c], c, codes[x], scales[x], w4, w4s)

        def bias4(x, c):
            ys[x, c] = work.tile([P, 512], F32, name="y", bufs=3)
            pairs_apart = "p (m u e) -> p u m e"
            nc.vector.tensor_tensor(
                out=ys[x, c][:].rearrange("p (u m e) -> p u m e", u=2, e=2), in0=accs[x, c][:].rearrange(pairs_apart, u=2, e=2),
                in1=b4_t[:, 512 * c:512 * (c + 1)].rearrange(pairs_apart, u=2, e=2), op=ALU.add)

        def leak4(x, c):
            if c == 0:
                h4[x] = work.tile([P, HID], BF16, name="h4", align_bytes=64)
            y = ys[x, c]
            nc.vector.scalar_tensor_tensor(out=h4[x][:, 512 * c:512 * (c + 1)], in0=y[:], scalar=SLOPE, in1=y[:], op0=ALU.mult, op1=ALU.max)

        def turn_h(x, gp):
            pair = bank([P, 2, 2, P], "pair4")
            for g in (2 * gp, 2 * gp + 1):
                turn(h4[x][:].bitcast(F32), g, pair, True)
            if gp == 0:
                grouped4[x] = work.tile([P, GROUPS, P, 4], BF16, name="grouped4", align_bytes=64)
            nc.scalar.copy(
                grouped4[x][:, 2 * gp:2 * gp + 2, :, :].rearrange("p g r t -> p (g r t)").bitcast(F32).rearrange("p (g r u) -> p g r u", g=2, u=2),
                pair[:].rearrange("p g u r -> p g r u"))

        def quant_h(x, g0=0, g1=GROUPS):
            if g0 == 0:
                codes4[x] = work.tile([P, GROUPS * P], U32, name="codes4", align_bytes=64)
                scales4[x] = work.tile([P, GROUPS * P], U8, name="scales4", align_bytes=64)
            cols = slice(P * g0, P * g1)
            nc.vector.quantize_mx(out=codes4[x][:, cols].bitcast(FP8X4), scales=scales4[x][:, cols], in_=grouped4[x][:, g0:g1, :, :].rearrange("p g r t -> p (g r t)"))

        def layer5(x, c):
            accs[x, c] = bank([P, 512], "acc2")
            layer(accs[x, c], c, codes4[x], scales4[x], w5, w5s)

        def bias5(x, c0, c1):
            if c0 == 0:
                zs[x] = work.tile([P, DOUT], F32, name="z", bufs=4)
                ns[x] = work.tile([P, DOUT], F32, name="n", bufs=4)
            nc.vector.tensor_tensor(out=zs[x][:, c0:c1], in0=accs[x, c0 // 512][:, c0 % 512:c0 % 512 + c1 - c0], in1=b5_t[:, c0:c1], op=ALU.add)

        def exp5(x, c0, c1, on_vector):
            z, n = zs[x][:, c0:c1], ns[x][:, c0:c1]
            if on_vector:
                nc.vector.scalar_tensor_tensor(out=n, in0=z, scalar=-1.0, in1=z, op0=ALU.mult, op1=ALU.min)
                nc.scalar.activation(n, n, ACTF.Exp)
            else:
                nc.scalar.activation(n, z, ACTF.Abs)
                nc.scalar.activation(n, n, ACTF.Exp, scale=-1.0)

        def log5(x, step=512):
            for c in range(0, DOUT, step):
                nc.scalar.activation(ns[x][:, c:c + step], ns[x][:, c:c + step], ACTF.Ln, bias=1.0)

        def soft5(x, step=512):
            for c in range(0, DOUT, step):
                cols = slice(c, c + step)
                nc.vector.scalar_tensor_tensor(out=A[x][:, cols], in0=zs[x][:, cols], scalar=FLOOR, in1=ns[x][:, cols], op0=ALU.max, op1=ALU.add)

        def flip5(x, on_vector):
            dst = AT[x][:].rearrange("p (a c i) -> p a i c", a=8, c=4)
            src = A[x][:].rearrange("p (i a c) -> p a i c", a=8, c=4)
            if on_vector:
                nc.vector.tensor_copy(out=dst, in_=src)
            else:
                nc.scalar.copy(dst, src)

        halves = 2 * ITERS
        lead = 0
        seq = []
        for b in range(halves + lead):
            for x in range(TILES):
                h = b if x < 2 else b - lead
                seq.append(h * TILES + x if 0 <= h < halves else None)
        at = [0]

        def advance(count):
            for p in range(at[0], at[0] + count):
                slot(p)
            at[0] += count

        prod, turned, sums, inv, turned_sb, rows_t = {}, {}, {}, {}, {}, {}

        def source(n):
            h, x = divmod(n, TILES)
            return A[x] if h % 2 == 0 else AT[x]

        def scale_vec(n, r0, r1):
            cols = slice(N * r0, N * r1)
            nc.vector.tensor_tensor(
                out=prod[n][:, cols].rearrange("p (a c) -> p a c", c=N), in0=source(n)[:, cols].rearrange("p (a c) -> p a c", c=N),
                in1=inv[n - TILES][:, r0:r1].unsqueeze(2).to_broadcast([P, r1 - r0, N]), op=ALU.mult)

        def scale_act(n, r0, r1):
            for a in range(r0, r1):
                cols = slice(N * a, N * (a + 1))
                nc.scalar.activation(prod[n][:, cols], source(n)[:, cols], ACTF.Copy, scale=inv[n - TILES][:, a:a + 1])

        def turn_chunk(n, k, first, last):
            nc.tensor.matmul(out=turned[n][:], lhsT=prod[n][:, P * k:P * (k + 1)], rhs=ident[:], is_transpose=True, start=first, stop=last)

        def take(n):
            turned_sb[n] = work.tile([P, P], F32, name="ts", bufs=4)
            nc.scalar.copy(turned_sb[n][:], turned[n][:])

        def fold_sum(n):
            width = WIDE if n < TILES else 128 if n < 2 * TILES else NARROW
            sums[n] = bank([P, width], "sums")
            nc.tensor.matmul(out=sums[n][:], lhsT=turned_sb[n][:], rhs=(fold_rows if n >= last else fold)[:, 0:width], start=True, stop=True)

        floor_of, half_inv = {}, {}
        exact = (halves - 2) * TILES

        def root_table():
            nc.scalar.activation(warm[:], warm[:], ACTF.Abs_reciprocal_sqrt)

        def clamp(n):
            floor_of[n] = work.tile([P, N], F32, name="floor", bufs=16)
            if n < 2 * TILES:
                nc.vector.tensor_scalar(out=floor_of[n][:], in0=sums[n][:, 0:N], scalar1=EPS, scalar2=None, op0=ALU.max)
            else:
                nc.vector.scalar_tensor_tensor(out=floor_of[n][:], in0=floor_of[n - 2 * TILES][:], scalar=EPS, in1=sums[n][:, 0:N], op0=ALU.mult, op1=ALU.max)

        def root(n):
            inv[n] = work.tile([P, N], F32, name="inv", bufs=16)
            if n >= exact:
                nc.vector.reciprocal(inv[n][:], floor_of[n][:])
                return
            half_inv[n] = work.tile([P, N], F32, name="half_inv", bufs=4)
            nc.scalar.activation(half_inv[n][:], floor_of[n][:], ACTF.Abs_reciprocal_sqrt)

        def square(n):
            if n < exact:
                nc.scalar.activation(inv[n][:], half_inv[n][:], ACTF.Square)

        last = (halves - 1) * TILES

        def row_scaled(n):
            rows_t[n] = work.tile([P, DOUT], F32, name="r", bufs=4)
            nc.vector.tensor_tensor(
                out=rows_t[n][:].rearrange("p (i j) -> p i j", j=N), in0=A[n % TILES][:].rearrange("p (i j) -> p i j", j=N),
                in1=inv[n - TILES][:].unsqueeze(1).to_broadcast([P, N, N]), op=ALU.mult)

        def turn_row(n, k):
            nc.tensor.matmul(out=turned[n][:], lhsT=rows_t[n][:, k:DOUT:8], rhs=ident[:], is_transpose=True, start=(k == 0), stop=(k == 7))

        def finish(n):
            r, u = rows_t[n], inv[n]
            o = work.tile([P, DOUT], F32, name="o", bufs=4)
            cut = 18
            where = out2[n % TILES * P:(n % TILES + 1) * P, :]
            nc.vector.tensor_tensor(out=o[:, 0:N * cut].rearrange("p (i j) -> p i j", j=N), in0=r[:, 0:N * cut].rearrange("p (i j) -> p i j", j=N), in1=u[:, 0:cut].unsqueeze(2).to_broadcast([P, cut, N]), op=ALU.mult)
            nc.sync.dma_start(out=where[:, 0:N * cut], in_=o[:, 0:N * cut])
            for a in range(cut, N):
                cols = slice(N * a, N * (a + 1))
                nc.scalar.activation(o[:, cols], r[:, cols], ACTF.Copy, scale=u[:, a:a + 1])
            nc.sync.dma_start(out=where[:, N * cut:], in_=o[:, N * cut:])

        def key(p):
            return seq[p] if 0 <= p < len(seq) else None

        def last_slot(p):
            n, n1, n2, n3 = key(p), key(p - 1), key(p - 2), key(p - 3)
            if n is not None:
                turned[n] = bank([P, P], "turned")
                row_scaled(n)
                for k in range(8):
                    turn_row(n, k)
            if n1 is not None:
                take(n1)
                fold_sum(n1)
            if n3 is not None:
                root(n3)
                square(n3)
                if n3 >= last:
                    finish(n3)
            if n2 is not None:
                clamp(n2)

        def slot(p):
            if p >= last:
                last_slot(p)
                return
            n, n1, n2, n3, n4 = key(p), key(p - 1), key(p - 2), key(p - 3), key(p - 4)
            live = n is not None
            full = live and n >= TILES
            if live:
                turned[n] = bank([P, P], "turned")
                prod[n] = work.tile([P, DOUT], F32, name="prod", bufs=4) if full else A[n]
            if full:
                scale_act(n, 28, 32)
            if live:
                turn_chunk(n, 7, True, False)
            if full:
                scale_vec(n, 0, 12)
            if live:
                turn_chunk(n, 1, False, False)
            if live:
                turn_chunk(n, 2, False, False)
            if n3 is not None:
                root(n3)
            if full:
                scale_vec(n, 12, 21)
            if full:
                scale_act(n, 24, 28)
            if live:
                turn_chunk(n, 6, False, False)
            if live:
                turn_chunk(n, 0, False, False)
            if live:
                turn_chunk(n, 4, False, False)
            if n2 is not None:
                clamp(n2)
            if n3 is not None:
                square(n3)
            if full:
                scale_act(n, 21, 24)
            if live:
                turn_chunk(n, 5, False, False)
            if live:
                turn_chunk(n, 3, False, True)
            if n1 is not None:
                take(n1)
            if n1 is not None:
                fold_sum(n1)

        for i in range(WIDE // N):
            nc.vector.tensor_reduce(out=fold[:, N * i:N * (i + 1)], in_=ident[:].rearrange("p (q j) -> p j q", q=4), axis=AX.X, op=ALU.add)
            nc.vector.tensor_reduce(out=fold_rows[:, N * i:N * (i + 1)], in_=ident[:].rearrange("p (i q) -> p i q", q=4), axis=AX.X, op=ALU.add)
        for g in range(GROUPS):
            widen(0, g, g % 2 == 1)
        turn_x(0, 0)
        turn_x(0, 1)
        for g in range(GROUPS):
            widen(1, g)
        for g in range(GROUPS):
            scale_x(0, g)
        turn_x(1, 0)
        turn_x(1, 1)
        quant_x(0, 0, 2)
        quant_x(0, 2, 4)
        scale_x(1, 0)
        scale_x(1, 1)
        layer4(0, 0)
        scale_x(1, 2)
        layer4(0, 1)
        bias4(0, 0)
        scale_x(1, 3)
        layer4(0, 2)
        leak4(0, 0)
        bias4(0, 1)
        quant_x(1)
        leak4(0, 1)
        layer4(0, 3)
        bias4(0, 2)
        for g in range(GROUPS):
            widen(2, g)
        turn_h(0, 0)
        turn_x(2, 0)
        turn_x(2, 1)
        bias4(0, 3)
        leak4(0, 2)
        leak4(0, 3)
        layer4(1, 0)
        turn_h(0, 1)
        layer4(1, 1)
        for g in range(GROUPS):
            widen(3, g)
        for x in (1, 2):
            scale_x(x + 1, 0)
            scale_x(x + 1, 1)
            scale_x(x + 1, 2)
            bias4(x, 0)
            quant_h(x - 1)
            scale_x(x + 1, 3)
            layer5(x - 1, 0)
            leak4(x, 0)
            bias4(x, 1)
            layer4(x, 2)
            quant_x(x + 1)
            leak4(x, 1)
            bias5(x - 1, 0, 512)
            exp5(x - 1, 0, 512, False)
            layer4(x, 3)
            bias4(x, 2)
            layer5(x - 1, 1)
            turn_h(x, 0)
            bias4(x, 3)
            leak4(x, 2)
            bias5(x - 1, 512, DOUT)
            exp5(x - 1, 512, DOUT, False)
            leak4(x, 3)
            if x == 1:
                turn_x(3, 0)
                turn_x(3, 1)
            layer4(x + 1, 0)
            turn_h(x, 1)
            layer4(x + 1, 1)
        bias4(3, 0)
        leak4(3, 0)
        quant_h(2)
        layer4(3, 2)
        bias4(3, 1)
        layer4(3, 3)
        bias4(3, 2)
        layer5(2, 0)
        log5(0)
        leak4(3, 1)
        bias4(3, 3)
        turn_h(3, 0)
        layer5(2, 1)
        leak4(3, 2)
        log5(1)
        leak4(3, 3)
        bias5(2, 0, 512)
        soft5(0)
        bias5(2, 512, DOUT)
        turn_h(3, 1)
        quant_h(3, 0, 2)
        quant_h(3, 2, 4)
        exp5(2, 512, DOUT, True)
        layer5(3, 0)
        soft5(1)
        bias5(3, 0, 256)
        exp5(2, 0, 512, True)
        bias5(3, 256, 512)
        exp5(3, 0, 256, True)
        layer5(3, 1)
        bias5(3, 512, 768)
        advance(2)
        exp5(3, 256, 512, True)
        bias5(3, 768, DOUT)
        exp5(3, 512, 768, True)
        exp5(3, 768, DOUT, True)
        flip5(0, True)
        flip5(1, True)
        log5(2)
        soft5(2)
        log5(3, 256)
        root_table()
        soft5(3, 256)
        flip5(2, True)
        flip5(3, True)
        advance(len(seq) + 4 - at[0])
